import numpy as np
import ml_dtypes


def mxq(x, axis, fmt="e4m3"):
    dtype, down = {"e4m3": (ml_dtypes.float8_e4m3fn, 7), "e5m2": (ml_dtypes.float8_e5m2, 14)}[fmt]
    v = np.moveaxis(np.asarray(x, np.float32).astype(ml_dtypes.bfloat16).astype(np.float64), axis, -1)
    blocks = v.reshape(v.shape[:-1] + (-1, 32))
    amax = np.abs(blocks).max(-1, keepdims=True)
    byte = np.maximum(np.where(amax > 0, np.frexp(amax)[1] - 1 + 127, 0) - down, 1)
    scale = np.exp2(byte - 127.0)
    codes = (blocks / scale).astype(np.float32).astype(dtype).astype(np.float64)
    return np.moveaxis((codes * scale).reshape(v.shape), -1, axis)


WIDE = False


def mx_kscale(k):
    if not WIDE:
        return np.ones(k)
    levels = np.array([10, -10, 5, -5, 0])
    a = np.random.permutation(np.resize(levels, k // 512 * 4)).reshape(k // 512, 4)
    idx = np.arange(k)
    return np.exp2(a[idx // 512, idx % 128 // 32])


BF16 = ml_dtypes.bfloat16


def bf(x):
    return np.asarray(x, np.float32).astype(BF16)


def f64(x):
    return np.asarray(x).astype(np.float64)


B, I, H, P = 8192, 256, 256, 2048
C = I + H


def sigmoid(v):
    return 1.0 / (1.0 + np.exp(-v))


def setup_inputs():
    s = mx_kscale(C)
    return {"x": bf(np.random.standard_normal((B, I)) * s[:I]),
            "rh": bf(np.random.standard_normal((B, H)) * 0.95 * s[I:]),
            "update": bf(np.random.standard_normal((B, H)) * 0.7),
            "hidden": bf(1.5 + np.random.standard_normal((B, H))),
            "Wn": bf(np.random.standard_normal((H, C)) / np.sqrt(C) / s[None, :]),
            "bn": bf(-0.1 + 0.2 * np.random.standard_normal(H)),
            "connection_strength": bf(1.0 + 0.3 * np.random.standard_normal(H)),
            "connection_decay": bf(0.4 + 0.2 * np.random.random(1)),
            "connection_history": bf(2.0 * np.random.standard_normal(H))}


def reference(x, rh, update, hidden, Wn, bn, connection_strength, connection_decay, connection_history):
    h = f64(hidden)
    u = f64(update)
    activity = np.mean(np.abs(h), axis=0)
    ch = f64(connection_history) * f64(connection_decay) + activity
    cs = f64(connection_strength) * sigmoid(ch)
    combined_reset = np.concatenate([f64(x), f64(rh)], axis=1)
    new = (mxq(combined_reset, 1, "e4m3") @ mxq(f64(Wn), 1, "e4m3").T) + f64(bn)
    return (1.0 - u) * h + u * new * cs[None, :]

@@ -1,0 +1,257 @@
+from contextlib import ExitStack
+
+import concourse.mybir as mybir
+from concourse.masks import make_identity
+
+F32 = mybir.dt.float32
+BF16 = mybir.dt.bfloat16
+I32 = mybir.dt.int32
+U32 = mybir.dt.uint32
+U8 = mybir.dt.uint8
+FP8X4 = mybir.dt.float8_e4m3fn_x4
+ALU = mybir.AluOpType
+ACT = mybir.ActivationFunctionType
+
+P = 128
+B = 8192
+H = 256
+HALVES = H // P
+ROW_TILES = B // P
+GROUP_TILES = 4
+GROUP_ROWS = GROUP_TILES * P
+GROUP_COLS = GROUP_TILES * H
+CHUNK_GROUPS = 2
+CHUNK_COLS = CHUNK_GROUPS * GROUP_COLS
+CHUNKS = ROW_TILES // (GROUP_TILES * CHUNK_GROUPS)
+BANK_TILES = 2
+ONES_COLS = 32
+ABS_MASK = 0x7FFF7FFF
+
+FLOPS = 2 * B * (2 * H) * H
+
+
+def tile_persistentgrucell_pb_t_kernel(
+    tc,
+    x,
+    rh,
+    update,
+    hidden,
+    Wn,
+    bn,
+    connection_strength,
+    connection_decay,
+    connection_history,
+    out,
+):
+    nc = tc.nc
+    x_rows = x.rearrange("(p t) k -> p (t k)", t=ROW_TILES)
+    rh_rows = rh.rearrange("(p t) k -> p (t k)", t=ROW_TILES)
+    u_rows = update.rearrange("(p t) k -> p (t k)", t=ROW_TILES)
+    h_rows = hidden.rearrange("(p t) k -> p (t k)", t=ROW_TILES)
+    out_rows = out.rearrange("(p t) k -> p (t k)", t=ROW_TILES)
+
+    with ExitStack() as ctx:
+        const = ctx.enter_context(tc.tile_pool(name="const", bufs=1))
+        h_pool = ctx.enter_context(tc.tile_pool(name="h_pool", bufs=1))
+        loads = ctx.enter_context(tc.tile_pool(name="loads", bufs=5))
+        blend = ctx.enter_context(tc.tile_pool(name="blend", bufs=5))
+        work = ctx.enter_context(tc.tile_pool(name="work", bufs=3))
+        psum = ctx.enter_context(tc.psum_pool(name="psum", bufs=2))
+
+        table_warm = const.tile([P, 1], F32)
+        nc.vector.memset(table_warm[:], 0.0)
+        nc.scalar.activation(out=table_warm[:], in_=table_warm[:], func=ACT.Sigmoid)
+        ident_f32 = const.tile([P, P], F32)
+        make_identity(nc, ident_f32[:])
+        ident_bf16 = const.tile([P, P], BF16)
+        make_identity(nc, ident_bf16[:])
+        ones = const.tile([P, ONES_COLS], BF16)
+        nc.vector.memset(ones[:], 1.0)
+
+        vec_rows = const.tile([P, P], BF16)
+        nc.vector.memset(vec_rows[:], 0.0)
+        for r, vec in enumerate((bn, connection_strength, connection_history)):
+            nc.scalar.dma_start(
+                out=vec_rows[HALVES * r : HALVES * (r + 1), :],
+                in_=vec.rearrange("(a c) -> a c", a=HALVES),
+            )
+        decay_bf16 = const.tile([P, 1], BF16)
+        nc.scalar.dma_start(out=decay_bf16[:], in_=connection_decay.partition_broadcast(P))
+        w_sb = const.tile([P, HALVES * 2 * H], BF16)
+        nc.scalar.dma_start(
+            out=w_sb[:].rearrange("p (a k) -> p a k", a=HALVES),
+            in_=Wn.rearrange("(a p) k -> p a k", p=P),
+        )
+
+        act_ps = [psum.tile([P, ONES_COLS], F32, tag="m_ps", name="act_ps%d" % a) for a in range(HALVES)]
+        h_sb = []
+        for c in range(CHUNKS):
+            h_chunk = h_pool.tile([P, CHUNK_COLS], BF16, name="h_chunk%d" % c)
+            h_sb.append(h_chunk)
+            nc.sync.dma_start(out=h_chunk[:], in_=h_rows[:, c * CHUNK_COLS : (c + 1) * CHUNK_COLS])
+            h_abs = work.tile([P, CHUNK_COLS], BF16)
+            nc.vector.tensor_scalar(
+                out=h_abs[:].bitcast(I32),
+                in0=h_chunk[:].bitcast(I32),
+                scalar1=ABS_MASK,
+                scalar2=None,
+                op0=ALU.bitwise_and,
+            )
+            blocks = CHUNK_COLS // P
+            for k in range(blocks):
+                nc.tensor.matmul(
+                    out=act_ps[k % HALVES][:],
+                    lhsT=h_abs[:, k * P : (k + 1) * P],
+                    rhs=ones[:],
+                    start=(c == 0 and k < HALVES),
+                    stop=(c == CHUNKS - 1 and k >= blocks - HALVES),
+                )
+
+        w_words = w_sb[:].bitcast(F32)
+        wt_ps = psum.tile([P, 2, H], F32, tag="xt_ps")
+        for a in range(HALVES):
+            for s in range(2):
+                nc.tensor.transpose(
+                    wt_ps[:, s, a * P : (a + 1) * P],
+                    w_words[:, (a * 2 + s) * P : (a * 2 + s + 1) * P],
+                    ident_f32[:],
+                )
+        w_grouped = const.tile([P, 4 * H], BF16, align_bytes=64)
+        nc.vector.tensor_copy(
+            out=w_grouped[:].bitcast(F32).rearrange("q (n s) -> q n s", s=2),
+            in_=wt_ps[:].rearrange("q s n -> q n s"),
+        )
+        w_codes = const.tile([P, H], U32, align_bytes=64)
+        w_scales = const.tile([P, H], U8, align_bytes=64)
+        nc.vector.quantize_mx(out=w_codes[:].bitcast(FP8X4), scales=w_scales[:], in_=w_grouped[:])
+
+        vec_ps = psum.tile([P, P], BF16, tag="ut_ps")
+        nc.tensor.transpose(vec_ps[:], vec_rows[:], ident_bf16[:])
+        vec_cols = const.tile([P, 3 * HALVES], F32)
+        nc.vector.tensor_copy(out=vec_cols[:], in_=vec_ps[:, 0 : 3 * HALVES])
+        bn_col = vec_cols[:, 0:HALVES]
+        strength_col = vec_cols[:, HALVES : 2 * HALVES]
+        history_col = vec_cols[:, 2 * HALVES : 3 * HALVES]
+        decay_col = const.tile([P, 1], F32)
+        nc.vector.tensor_copy(out=decay_col[:], in_=decay_bf16[:])
+        decayed = const.tile([P, HALVES], F32)
+        nc.vector.tensor_scalar(
+            out=decayed[:], in0=history_col, scalar1=decay_col[:, 0:1], scalar2=None, op0=ALU.mult
+        )
+        gate = const.tile([P, HALVES], F32)
+        for a in range(HALVES):
+            nc.scalar.activation(
+                out=gate[:, a : a + 1],
+                in_=act_ps[a][:, 0:1],
+                func=ACT.Sigmoid,
+                bias=decayed[:, a : a + 1],
+                scale=1.0 / B,
+            )
+        cs_col = const.tile([P, HALVES], F32)
+        nc.vector.tensor_tensor(out=cs_col[:], in0=strength_col, in1=gate[:], op=ALU.mult)
+
+        for c in range(CHUNKS):
+            chunk_cols = slice(c * CHUNK_COLS, (c + 1) * CHUNK_COLS)
+            u_chunk = loads.tile([P, CHUNK_COLS], BF16)
+            nc.sync.dma_start(out=u_chunk[:], in_=u_rows[:, chunk_cols])
+            x_chunk = loads.tile([P, CHUNK_COLS], BF16)
+            nc.sync.dma_start(out=x_chunk[:], in_=x_rows[:, chunk_cols])
+            rh_chunk = loads.tile([P, CHUNK_COLS], BF16)
+            nc.sync.dma_start(out=rh_chunk[:], in_=rh_rows[:, chunk_cols])
+            x_words = x_chunk[:].bitcast(F32)
+            rh_words = rh_chunk[:].bitcast(F32)
+            kept = blend.tile([P, CHUNK_COLS], F32)
+
+            for gi in range(CHUNK_GROUPS):
+                g = c * CHUNK_GROUPS + gi
+                group_cols = slice(gi * GROUP_COLS, (gi + 1) * GROUP_COLS)
+
+                one_minus_u = work.tile([P, GROUP_COLS], F32)
+                if g % 2 == 0:
+                    nc.scalar.activation(
+                        out=one_minus_u[:], in_=u_chunk[:, group_cols], func=ACT.Copy, bias=1.0, scale=-1.0
+                    )
+                else:
+                    nc.gpsimd.tensor_scalar(
+                        out=one_minus_u[:],
+                        in0=u_chunk[:, group_cols],
+                        scalar1=-1.0,
+                        scalar2=1.0,
+                        op0=ALU.mult,
+                        op1=ALU.add,
+                    )
+                nc.gpsimd.tensor_tensor(
+                    out=kept[:, group_cols], in0=one_minus_u[:], in1=h_sb[c][:, group_cols], op=ALU.mult
+                )
+
+                grouped = work.tile([P, 4 * GROUP_ROWS], BF16, align_bytes=64)
+                grouped_words = grouped[:].bitcast(F32).rearrange("q (n s) -> q n s", s=2)
+                for j in range(GROUP_TILES // BANK_TILES):
+                    xt_ps = psum.tile([P, 2, BANK_TILES * P], F32)
+                    for i in range(BANK_TILES):
+                        t = gi * GROUP_TILES + j * BANK_TILES + i
+                        nc.tensor.transpose(
+                            xt_ps[:, 0, i * P : (i + 1) * P], x_words[:, t * P : (t + 1) * P], ident_f32[:]
+                        )
+                        nc.tensor.transpose(
+                            xt_ps[:, 1, i * P : (i + 1) * P], rh_words[:, t * P : (t + 1) * P], ident_f32[:]
+                        )
+                    nc.scalar.copy(
+                        out=grouped_words[:, j * BANK_TILES * P : (j + 1) * BANK_TILES * P, :],
+                        in_=xt_ps[:].rearrange("q s n -> q n s"),
+                    )
+                codes = work.tile([P, GROUP_ROWS], U32, align_bytes=64)
+                scales = work.tile([P, GROUP_ROWS], U8, align_bytes=64)
+                nc.vector.quantize_mx(out=codes[:].bitcast(FP8X4), scales=scales[:], in_=grouped[:])
+
+                ut_ps = psum.tile([P, HALVES, GROUP_ROWS], BF16)
+                for i in range(GROUP_TILES):
+                    for a in range(HALVES):
+                        col = (gi * GROUP_TILES + i) * H + a * P
+                        nc.tensor.transpose(
+                            ut_ps[:, a, i * P : (i + 1) * P], u_chunk[:, col : col + P], ident_bf16[:]
+                        )
+                u_cs = work.tile([P, HALVES, GROUP_ROWS], F32)
+                for a in range(HALVES):
+                    nc.scalar.activation(
+                        out=u_cs[:, a, :], in_=ut_ps[:, a, :], func=ACT.Copy, scale=cs_col[:, a : a + 1]
+                    )
+
+                gated = work.tile([P, HALVES, GROUP_ROWS], F32)
+                for a in range(HALVES):
+                    acc_ps = psum.tile([P, GROUP_ROWS], F32)
+                    nc.tensor.matmul_mx(
+                        out=acc_ps[:],
+                        lhsT=w_codes[:, a * P : (a + 1) * P].bitcast(FP8X4),
+                        lhsT_scale=w_scales[:, a * P : (a + 1) * P],
+                        rhs=codes[:].bitcast(FP8X4),
+                        rhs_scale=scales[:],
+                        start=True,
+                        stop=True,
+                    )
+                    nc.vector.scalar_tensor_tensor(
+                        out=gated[:, a, :],
+                        in0=acc_ps[:],
+                        scalar=bn_col[:, a : a + 1],
+                        in1=u_cs[:, a, :],
+                        op0=ALU.add,
+                        op1=ALU.mult,
+                    )
+
+                for j in range(GROUP_TILES // BANK_TILES):
+                    m_ps = psum.tile([P, BANK_TILES * H], F32)
+                    for i in range(BANK_TILES):
+                        n0 = (j * BANK_TILES + i) * P
+                        for a in range(HALVES):
+                            nc.tensor.transpose(
+                                m_ps[:, i * H + a * P : i * H + (a + 1) * P], gated[:, a, n0 : n0 + P], ident_f32[:]
+                            )
+                    bank_cols = slice(
+                        gi * GROUP_COLS + j * BANK_TILES * H, gi * GROUP_COLS + (j + 1) * BANK_TILES * H
+                    )
+                    nc.vector.tensor_tensor(
+                        out=kept[:, bank_cols], in0=m_ps[:], in1=kept[:, bank_cols], op=ALU.add
+                    )
+                nc.sync.dma_start(
+                    out=out_rows[:, g * GROUP_COLS : (g + 1) * GROUP_COLS], in_=kept[:, group_cols]
+                )

@@ -83,7 +83,7 @@ def tile_persistentgrucell_pb_t_kernel(
             in_=Wn.rearrange("(a p) k -> p a k", p=P),
         )
 
-        act_ps = [psum.tile([P, ONES_COLS], F32, tag="m_ps", name="act_ps%d" % a) for a in range(HALVES)]
+        act_ps = [psum.tile([P, ONES_COLS], F32, tag="s_ps", bufs=4, name="act_ps%d" % a) for a in range(HALVES)]
         h_sb = []
         for c in range(CHUNKS):
             h_chunk = h_pool.tile([P, CHUNK_COLS], BF16, name="h_chunk%d" % c)
@@ -125,7 +125,7 @@ def tile_persistentgrucell_pb_t_kernel(
         w_scales = const.tile([P, H], U8, align_bytes=64)
         nc.vector.quantize_mx(out=w_codes[:].bitcast(FP8X4), scales=w_scales[:], in_=w_grouped[:])
 
-        vec_ps = psum.tile([P, P], BF16, tag="ut_ps")
+        vec_ps = psum.tile([P, P], BF16, tag="acc_ps")
         nc.tensor.transpose(vec_ps[:], vec_rows[:], ident_bf16[:])
         vec_cols = const.tile([P, 3 * HALVES], F32)
         nc.vector.tensor_copy(out=vec_cols[:], in_=vec_ps[:, 0 : 3 * HALVES])
@@ -149,6 +149,8 @@ def tile_persistentgrucell_pb_t_kernel(
             )
         cs_col = const.tile([P, HALVES], F32)
         nc.vector.tensor_tensor(out=cs_col[:], in0=strength_col, in1=gate[:], op=ALU.mult)
+        bias_col = const.tile([P, HALVES], F32)
+        nc.vector.tensor_tensor(out=bias_col[:], in0=bn_col, in1=cs_col[:], op=ALU.mult)
 
         for c in range(CHUNKS):
             chunk_cols = slice(c * CHUNK_COLS, (c + 1) * CHUNK_COLS)
@@ -160,29 +162,20 @@ def tile_persistentgrucell_pb_t_kernel(
             nc.sync.dma_start(out=rh_chunk[:], in_=rh_rows[:, chunk_cols])
             x_words = x_chunk[:].bitcast(F32)
             rh_words = rh_chunk[:].bitcast(F32)
-            kept = blend.tile([P, CHUNK_COLS], F32)
+
+            blend_chunk = blend.tile([P, CHUNK_COLS], F32)
+            nc.vector.scalar_tensor_tensor(
+                out=blend_chunk[:],
+                in0=u_chunk[:],
+                scalar=1.0,
+                in1=h_sb[c][:],
+                op0=ALU.subtract,
+                op1=ALU.mult,
+            )
 
             for gi in range(CHUNK_GROUPS):
                 g = c * CHUNK_GROUPS + gi
                 group_cols = slice(gi * GROUP_COLS, (gi + 1) * GROUP_COLS)
-
-                one_minus_u = work.tile([P, GROUP_COLS], F32)
-                if g % 2 == 0:
-                    nc.scalar.activation(
-                        out=one_minus_u[:], in_=u_chunk[:, group_cols], func=ACT.Copy, bias=1.0, scale=-1.0
-                    )
-                else:
-                    nc.gpsimd.tensor_scalar(
-                        out=one_minus_u[:],
-                        in0=u_chunk[:, group_cols],
-                        scalar1=-1.0,
-                        scalar2=1.0,
-                        op0=ALU.mult,
-                        op1=ALU.add,
-                    )
-                nc.gpsimd.tensor_tensor(
-                    out=kept[:, group_cols], in0=one_minus_u[:], in1=h_sb[c][:, group_cols], op=ALU.mult
-                )
 
                 grouped = work.tile([P, 4 * GROUP_ROWS], BF16, align_bytes=64)
                 grouped_words = grouped[:].bitcast(F32).rearrange("q (n s) -> q n s", s=2)
@@ -204,20 +197,7 @@ def tile_persistentgrucell_pb_t_kernel(
                 scales = work.tile([P, GROUP_ROWS], U8, align_bytes=64)
                 nc.vector.quantize_mx(out=codes[:].bitcast(FP8X4), scales=scales[:], in_=grouped[:])
 
-                ut_ps = psum.tile([P, HALVES, GROUP_ROWS], BF16)
-                for i in range(GROUP_TILES):
-                    for a in range(HALVES):
-                        col = (gi * GROUP_TILES + i) * H + a * P
-                        nc.tensor.transpose(
-                            ut_ps[:, a, i * P : (i + 1) * P], u_chunk[:, col : col + P], ident_bf16[:]
-                        )
-                u_cs = work.tile([P, HALVES, GROUP_ROWS], F32)
-                for a in range(HALVES):
-                    nc.scalar.activation(
-                        out=u_cs[:, a, :], in_=ut_ps[:, a, :], func=ACT.Copy, scale=cs_col[:, a : a + 1]
-                    )
-
-                gated = work.tile([P, HALVES, GROUP_ROWS], F32)
+                scaled = work.tile([P, HALVES, GROUP_ROWS], F32)
                 for a in range(HALVES):
                     acc_ps = psum.tile([P, GROUP_ROWS], F32)
                     nc.tensor.matmul_mx(
@@ -229,29 +209,33 @@ def tile_persistentgrucell_pb_t_kernel(
                         start=True,
                         stop=True,
                     )
-                    nc.vector.scalar_tensor_tensor(
-                        out=gated[:, a, :],
-                        in0=acc_ps[:],
-                        scalar=bn_col[:, a : a + 1],
-                        in1=u_cs[:, a, :],
-                        op0=ALU.add,
-                        op1=ALU.mult,
+                    nc.scalar.activation(
+                        out=scaled[:, a, :],
+                        in_=acc_ps[:],
+                        func=ACT.Identity,
+                        bias=bias_col[:, a : a + 1],
+                        scale=cs_col[:, a : a + 1],
                     )
 
+                gated = work.tile([P, GROUP_COLS], F32)
                 for j in range(GROUP_TILES // BANK_TILES):
-                    m_ps = psum.tile([P, BANK_TILES * H], F32)
+                    s_ps = psum.tile([P, BANK_TILES * H], F32, bufs=4)
                     for i in range(BANK_TILES):
                         n0 = (j * BANK_TILES + i) * P
                         for a in range(HALVES):
                             nc.tensor.transpose(
-                                m_ps[:, i * H + a * P : i * H + (a + 1) * P], gated[:, a, n0 : n0 + P], ident_f32[:]
+                                s_ps[:, i * H + a * P : i * H + (a + 1) * P], scaled[:, a, n0 : n0 + P], ident_f32[:]
                             )
-                    bank_cols = slice(
-                        gi * GROUP_COLS + j * BANK_TILES * H, gi * GROUP_COLS + (j + 1) * BANK_TILES * H
-                    )
+                    bank = slice(j * BANK_TILES * H, (j + 1) * BANK_TILES * H)
                     nc.vector.tensor_tensor(
-                        out=kept[:, bank_cols], in0=m_ps[:], in1=kept[:, bank_cols], op=ALU.add
+                        out=gated[:, bank],
+                        in0=s_ps[:],
+                        in1=u_chunk[:, gi * GROUP_COLS + j * BANK_TILES * H : gi * GROUP_COLS + (j + 1) * BANK_TILES * H],
+                        op=ALU.mult,
                     )
+                nc.vector.tensor_tensor(
+                    out=blend_chunk[:, group_cols], in0=gated[:], in1=blend_chunk[:, group_cols], op=ALU.subtract
+                )
                 nc.sync.dma_start(
-                    out=out_rows[:, g * GROUP_COLS : (g + 1) * GROUP_COLS], in_=kept[:, group_cols]
+                    out=out_rows[:, g * GROUP_COLS : (g + 1) * GROUP_COLS], in_=blend_chunk[:, group_cols]
                 )

@@ -5,7 +5,6 @@ from concourse.masks import make_identity
 
 F32 = mybir.dt.float32
 BF16 = mybir.dt.bfloat16
-I32 = mybir.dt.int32
 U32 = mybir.dt.uint32
 U8 = mybir.dt.uint8
 FP8X4 = mybir.dt.float8_e4m3fn_x4
@@ -25,7 +24,6 @@ CHUNK_COLS = CHUNK_GROUPS * GROUP_COLS
 CHUNKS = ROW_TILES // (GROUP_TILES * CHUNK_GROUPS)
 BANK_TILES = 2
 ONES_COLS = 32
-ABS_MASK = 0x7FFF7FFF
 
 FLOPS = 2 * B * (2 * H) * H
 
@@ -52,15 +50,14 @@ def tile_persistentgrucell_pb_t_kernel(
 
     with ExitStack() as ctx:
         const = ctx.enter_context(tc.tile_pool(name="const", bufs=1))
-        h_pool = ctx.enter_context(tc.tile_pool(name="h_pool", bufs=1))
-        loads = ctx.enter_context(tc.tile_pool(name="loads", bufs=5))
-        blend = ctx.enter_context(tc.tile_pool(name="blend", bufs=5))
+        keep = ctx.enter_context(tc.tile_pool(name="keep", bufs=1))
+        loads = ctx.enter_context(tc.tile_pool(name="loads", bufs=4))
         work = ctx.enter_context(tc.tile_pool(name="work", bufs=3))
         psum = ctx.enter_context(tc.psum_pool(name="psum", bufs=2))
 
         table_warm = const.tile([P, 1], F32)
         nc.vector.memset(table_warm[:], 0.0)
-        nc.scalar.activation(out=table_warm[:], in_=table_warm[:], func=ACT.Sigmoid)
+        nc.scalar.activation(out=table_warm[:], in_=table_warm[:], func=ACT.Tanh)
         ident_f32 = const.tile([P, P], F32)
         make_identity(nc, ident_f32[:])
         ident_bf16 = const.tile([P, P], BF16)
@@ -82,30 +79,6 @@ def tile_persistentgrucell_pb_t_kernel(
             out=w_sb[:].rearrange("p (a k) -> p a k", a=HALVES),
             in_=Wn.rearrange("(a p) k -> p a k", p=P),
         )
-
-        act_ps = [psum.tile([P, ONES_COLS], F32, tag="s_ps", bufs=4, name="act_ps%d" % a) for a in range(HALVES)]
-        h_sb = []
-        for c in range(CHUNKS):
-            h_chunk = h_pool.tile([P, CHUNK_COLS], BF16, name="h_chunk%d" % c)
-            h_sb.append(h_chunk)
-            nc.sync.dma_start(out=h_chunk[:], in_=h_rows[:, c * CHUNK_COLS : (c + 1) * CHUNK_COLS])
-            h_abs = work.tile([P, CHUNK_COLS], BF16)
-            nc.vector.tensor_scalar(
-                out=h_abs[:].bitcast(I32),
-                in0=h_chunk[:].bitcast(I32),
-                scalar1=ABS_MASK,
-                scalar2=None,
-                op0=ALU.bitwise_and,
-            )
-            blocks = CHUNK_COLS // P
-            for k in range(blocks):
-                nc.tensor.matmul(
-                    out=act_ps[k % HALVES][:],
-                    lhsT=h_abs[:, k * P : (k + 1) * P],
-                    rhs=ones[:],
-                    start=(c == 0 and k < HALVES),
-                    stop=(c == CHUNKS - 1 and k >= blocks - HALVES),
-                )
 
         w_words = w_sb[:].bitcast(F32)
         wt_ps = psum.tile([P, 2, H], F32, tag="xt_ps")
@@ -134,28 +107,63 @@ def tile_persistentgrucell_pb_t_kernel(
         history_col = vec_cols[:, 2 * HALVES : 3 * HALVES]
         decay_col = const.tile([P, 1], F32)
         nc.vector.tensor_copy(out=decay_col[:], in_=decay_bf16[:])
-        decayed = const.tile([P, HALVES], F32)
+        half_decayed = const.tile([P, HALVES], F32)
         nc.vector.tensor_scalar(
-            out=decayed[:], in0=history_col, scalar1=decay_col[:, 0:1], scalar2=None, op0=ALU.mult
+            out=half_decayed[:], in0=history_col, scalar1=decay_col[:, 0:1], scalar2=0.5, op0=ALU.mult, op1=ALU.mult
         )
-        gate = const.tile([P, HALVES], F32)
+        half_strength = const.tile([P, HALVES], F32)
+        nc.vector.tensor_scalar(out=half_strength[:], in0=strength_col, scalar1=0.5, scalar2=None, op0=ALU.mult)
+
+        act_ps = [psum.tile([P, ONES_COLS], F32, tag="s_ps", bufs=4, name="act_ps%d" % a) for a in range(HALVES)]
+        u_sb = []
+        blend_sb = []
+        for c in range(CHUNKS):
+            chunk_cols = slice(c * CHUNK_COLS, (c + 1) * CHUNK_COLS)
+            h_chunk = loads.tile([P, CHUNK_COLS], BF16)
+            nc.sync.dma_start(out=h_chunk[:], in_=h_rows[:, chunk_cols])
+            u_chunk = keep.tile([P, CHUNK_COLS], BF16, name="u_chunk%d" % c)
+            u_sb.append(u_chunk)
+            nc.sync.dma_start(out=u_chunk[:], in_=u_rows[:, chunk_cols])
+            h_abs = work.tile([P, CHUNK_COLS], BF16)
+            nc.scalar.activation(out=h_abs[:], in_=h_chunk[:], func=ACT.Abs)
+            blocks = CHUNK_COLS // P
+            for k in range(blocks):
+                nc.tensor.matmul(
+                    out=act_ps[k % HALVES][:],
+                    lhsT=h_abs[:, k * P : (k + 1) * P],
+                    rhs=ones[:],
+                    start=(c == 0 and k < HALVES),
+                    stop=(c == CHUNKS - 1 and k >= blocks - HALVES),
+                )
+            blend_chunk = keep.tile([P, CHUNK_COLS], F32, name="blend_chunk%d" % c)
+            blend_sb.append(blend_chunk)
+            nc.vector.scalar_tensor_tensor(
+                out=blend_chunk[:],
+                in0=u_chunk[:],
+                scalar=1.0,
+                in1=h_chunk[:],
+                op0=ALU.subtract,
+                op1=ALU.mult,
+            )
+
+        tanh_col = const.tile([P, HALVES], F32)
         for a in range(HALVES):
             nc.scalar.activation(
-                out=gate[:, a : a + 1],
+                out=tanh_col[:, a : a + 1],
                 in_=act_ps[a][:, 0:1],
-                func=ACT.Sigmoid,
-                bias=decayed[:, a : a + 1],
-                scale=1.0 / B,
+                func=ACT.Tanh,
+                bias=half_decayed[:, a : a + 1],
+                scale=0.5 / B,
             )
         cs_col = const.tile([P, HALVES], F32)
-        nc.vector.tensor_tensor(out=cs_col[:], in0=strength_col, in1=gate[:], op=ALU.mult)
+        nc.vector.scalar_tensor_tensor(
+            out=cs_col[:], in0=tanh_col[:], scalar=1.0, in1=half_strength[:], op0=ALU.add, op1=ALU.mult
+        )
         bias_col = const.tile([P, HALVES], F32)
         nc.vector.tensor_tensor(out=bias_col[:], in0=bn_col, in1=cs_col[:], op=ALU.mult)
 
         for c in range(CHUNKS):
             chunk_cols = slice(c * CHUNK_COLS, (c + 1) * CHUNK_COLS)
-            u_chunk = loads.tile([P, CHUNK_COLS], BF16)
-            nc.sync.dma_start(out=u_chunk[:], in_=u_rows[:, chunk_cols])
             x_chunk = loads.tile([P, CHUNK_COLS], BF16)
             nc.sync.dma_start(out=x_chunk[:], in_=x_rows[:, chunk_cols])
             rh_chunk = loads.tile([P, CHUNK_COLS], BF16)
@@ -163,15 +171,8 @@ def tile_persistentgrucell_pb_t_kernel(
             x_words = x_chunk[:].bitcast(F32)
             rh_words = rh_chunk[:].bitcast(F32)
 
-            blend_chunk = blend.tile([P, CHUNK_COLS], F32)
-            nc.vector.scalar_tensor_tensor(
-                out=blend_chunk[:],
-                in0=u_chunk[:],
-                scalar=1.0,
-                in1=h_sb[c][:],
-                op0=ALU.subtract,
-                op1=ALU.mult,
-            )
+            u_chunk = u_sb[c]
+            blend_chunk = blend_sb[c]
 
             for gi in range(CHUNK_GROUPS):
                 g = c * CHUNK_GROUPS + gi

@@ -23,7 +23,10 @@ CHUNK_GROUPS = 2
 CHUNK_COLS = CHUNK_GROUPS * GROUP_COLS
 CHUNKS = ROW_TILES // (GROUP_TILES * CHUNK_GROUPS)
 BANK_TILES = 2
-ONES_COLS = 32
+GROUPS = ROW_TILES // GROUP_TILES
+LOAD_BUFS = 4
+ONES_COLS = 2
+MATMUL_EVERY = 3
 
 FLOPS = 2 * B * (2 * H) * H
 
@@ -51,19 +54,10 @@ def tile_persistentgrucell_pb_t_kernel(
     with ExitStack() as ctx:
         const = ctx.enter_context(tc.tile_pool(name="const", bufs=1))
         keep = ctx.enter_context(tc.tile_pool(name="keep", bufs=1))
-        loads = ctx.enter_context(tc.tile_pool(name="loads", bufs=4))
+        loads = ctx.enter_context(tc.tile_pool(name="loads", bufs=LOAD_BUFS))
         work = ctx.enter_context(tc.tile_pool(name="work", bufs=3))
         psum = ctx.enter_context(tc.psum_pool(name="psum", bufs=2))
-
-        table_warm = const.tile([P, 1], F32)
-        nc.vector.memset(table_warm[:], 0.0)
-        nc.scalar.activation(out=table_warm[:], in_=table_warm[:], func=ACT.Tanh)
-        ident_f32 = const.tile([P, P], F32)
-        make_identity(nc, ident_f32[:])
-        ident_bf16 = const.tile([P, P], BF16)
-        make_identity(nc, ident_bf16[:])
-        ones = const.tile([P, ONES_COLS], BF16)
-        nc.vector.memset(ones[:], 1.0)
+        ctx.enter_context(tc.manual_schedule())
 
         vec_rows = const.tile([P, P], BF16)
         nc.vector.memset(vec_rows[:], 0.0)
@@ -75,10 +69,19 @@ def tile_persistentgrucell_pb_t_kernel(
         decay_bf16 = const.tile([P, 1], BF16)
         nc.scalar.dma_start(out=decay_bf16[:], in_=connection_decay.partition_broadcast(P))
         w_sb = const.tile([P, HALVES * 2 * H], BF16)
-        nc.scalar.dma_start(
+        nc.sync.dma_start(
             out=w_sb[:].rearrange("p (a k) -> p a k", a=HALVES),
             in_=Wn.rearrange("(a p) k -> p a k", p=P),
         )
+        table_warm = const.tile([P, 1], F32)
+        nc.vector.memset(table_warm[:], 0.0)
+        nc.scalar.activation(out=table_warm[:], in_=table_warm[:], func=ACT.Tanh)
+        ident_f32 = const.tile([P, P], F32)
+        make_identity(nc, ident_f32[:])
+        ident_bf16 = const.tile([P, P], BF16)
+        make_identity(nc, ident_bf16[:])
+        ones = const.tile([P, ONES_COLS], BF16)
+        nc.vector.memset(ones[:], 1.0)
 
         w_words = w_sb[:].bitcast(F32)
         wt_ps = psum.tile([P, 2, H], F32, tag="xt_ps")
@@ -119,7 +122,7 @@ def tile_persistentgrucell_pb_t_kernel(
         blend_sb = []
         for c in range(CHUNKS):
             chunk_cols = slice(c * CHUNK_COLS, (c + 1) * CHUNK_COLS)
-            h_chunk = loads.tile([P, CHUNK_COLS], BF16)
+            h_chunk = keep.tile([P, CHUNK_COLS], BF16, name="h_chunk%d" % c)
             nc.sync.dma_start(out=h_chunk[:], in_=h_rows[:, chunk_cols])
             u_chunk = keep.tile([P, CHUNK_COLS], BF16, name="u_chunk%d" % c)
             u_sb.append(u_chunk)
@@ -162,81 +165,110 @@ def tile_persistentgrucell_pb_t_kernel(
         bias_col = const.tile([P, HALVES], F32)
         nc.vector.tensor_tensor(out=bias_col[:], in0=bn_col, in1=cs_col[:], op=ALU.mult)
 
-        for c in range(CHUNKS):
+        x_words = {}
+        rh_words = {}
+        grouped_of = {}
+        codes_of = {}
+        scales_of = {}
+        scaled_of = {}
+        gated_of = {}
+
+        def load_inputs(c):
             chunk_cols = slice(c * CHUNK_COLS, (c + 1) * CHUNK_COLS)
             x_chunk = loads.tile([P, CHUNK_COLS], BF16)
             nc.sync.dma_start(out=x_chunk[:], in_=x_rows[:, chunk_cols])
             rh_chunk = loads.tile([P, CHUNK_COLS], BF16)
             nc.sync.dma_start(out=rh_chunk[:], in_=rh_rows[:, chunk_cols])
-            x_words = x_chunk[:].bitcast(F32)
-            rh_words = rh_chunk[:].bitcast(F32)
+            x_words[c] = x_chunk[:].bitcast(F32)
+            rh_words[c] = rh_chunk[:].bitcast(F32)
 
-            u_chunk = u_sb[c]
-            blend_chunk = blend_sb[c]
-
-            for gi in range(CHUNK_GROUPS):
-                g = c * CHUNK_GROUPS + gi
-                group_cols = slice(gi * GROUP_COLS, (gi + 1) * GROUP_COLS)
-
+        def transpose_inputs(g, j):
+            c, gi = divmod(g, CHUNK_GROUPS)
+            if j == 0:
                 grouped = work.tile([P, 4 * GROUP_ROWS], BF16, align_bytes=64)
-                grouped_words = grouped[:].bitcast(F32).rearrange("q (n s) -> q n s", s=2)
-                for j in range(GROUP_TILES // BANK_TILES):
-                    xt_ps = psum.tile([P, 2, BANK_TILES * P], F32)
-                    for i in range(BANK_TILES):
-                        t = gi * GROUP_TILES + j * BANK_TILES + i
-                        nc.tensor.transpose(
-                            xt_ps[:, 0, i * P : (i + 1) * P], x_words[:, t * P : (t + 1) * P], ident_f32[:]
-                        )
-                        nc.tensor.transpose(
-                            xt_ps[:, 1, i * P : (i + 1) * P], rh_words[:, t * P : (t + 1) * P], ident_f32[:]
-                        )
-                    nc.scalar.copy(
-                        out=grouped_words[:, j * BANK_TILES * P : (j + 1) * BANK_TILES * P, :],
-                        in_=xt_ps[:].rearrange("q s n -> q n s"),
-                    )
-                codes = work.tile([P, GROUP_ROWS], U32, align_bytes=64)
-                scales = work.tile([P, GROUP_ROWS], U8, align_bytes=64)
-                nc.vector.quantize_mx(out=codes[:].bitcast(FP8X4), scales=scales[:], in_=grouped[:])
+                grouped_of[g] = grouped
+            grouped_words = grouped_of[g][:].bitcast(F32).rearrange("q (n s) -> q n s", s=2)
+            xt_ps = psum.tile([P, 2, BANK_TILES * P], F32)
+            for i in range(BANK_TILES):
+                t = gi * GROUP_TILES + j * BANK_TILES + i
+                nc.tensor.transpose(xt_ps[:, 0, i * P : (i + 1) * P], x_words[c][:, t * P : (t + 1) * P], ident_f32[:])
+                nc.tensor.transpose(xt_ps[:, 1, i * P : (i + 1) * P], rh_words[c][:, t * P : (t + 1) * P], ident_f32[:])
+            nc.scalar.copy(
+                out=grouped_words[:, j * BANK_TILES * P : (j + 1) * BANK_TILES * P, :],
+                in_=xt_ps[:].rearrange("q s n -> q n s"),
+            )
 
-                scaled = work.tile([P, HALVES, GROUP_ROWS], F32)
-                for a in range(HALVES):
-                    acc_ps = psum.tile([P, GROUP_ROWS], F32)
-                    nc.tensor.matmul_mx(
-                        out=acc_ps[:],
-                        lhsT=w_codes[:, a * P : (a + 1) * P].bitcast(FP8X4),
-                        lhsT_scale=w_scales[:, a * P : (a + 1) * P],
-                        rhs=codes[:].bitcast(FP8X4),
-                        rhs_scale=scales[:],
-                        start=True,
-                        stop=True,
-                    )
-                    nc.scalar.activation(
-                        out=scaled[:, a, :],
-                        in_=acc_ps[:],
-                        func=ACT.Identity,
-                        bias=bias_col[:, a : a + 1],
-                        scale=cs_col[:, a : a + 1],
-                    )
+        def quantise(g):
+            codes = work.tile([P, GROUP_ROWS], U32, align_bytes=64)
+            scales = work.tile([P, GROUP_ROWS], U8, align_bytes=64)
+            nc.vector.quantize_mx(out=codes[:].bitcast(FP8X4), scales=scales[:], in_=grouped_of[g][:])
+            codes_of[g] = codes
+            scales_of[g] = scales
 
+        def multiply(g):
+            scaled = work.tile([P, HALVES, GROUP_ROWS], F32)
+            for a in range(HALVES):
+                acc_ps = psum.tile([P, GROUP_ROWS], F32)
+                nc.tensor.matmul_mx(
+                    out=acc_ps[:],
+                    lhsT=w_codes[:, a * P : (a + 1) * P].bitcast(FP8X4),
+                    lhsT_scale=w_scales[:, a * P : (a + 1) * P],
+                    rhs=codes_of[g][:].bitcast(FP8X4),
+                    rhs_scale=scales_of[g][:],
+                    start=True,
+                    stop=True,
+                )
+                nc.scalar.activation(
+                    out=scaled[:, a, :],
+                    in_=acc_ps[:],
+                    func=ACT.Identity,
+                    bias=bias_col[:, a : a + 1],
+                    scale=cs_col[:, a : a + 1],
+                )
+            scaled_of[g] = scaled
+
+        def gate_rows(g, j):
+            c, gi = divmod(g, CHUNK_GROUPS)
+            if j == 0:
                 gated = work.tile([P, GROUP_COLS], F32)
-                for j in range(GROUP_TILES // BANK_TILES):
-                    s_ps = psum.tile([P, BANK_TILES * H], F32, bufs=4)
-                    for i in range(BANK_TILES):
-                        n0 = (j * BANK_TILES + i) * P
-                        for a in range(HALVES):
-                            nc.tensor.transpose(
-                                s_ps[:, i * H + a * P : i * H + (a + 1) * P], scaled[:, a, n0 : n0 + P], ident_f32[:]
-                            )
-                    bank = slice(j * BANK_TILES * H, (j + 1) * BANK_TILES * H)
-                    nc.vector.tensor_tensor(
-                        out=gated[:, bank],
-                        in0=s_ps[:],
-                        in1=u_chunk[:, gi * GROUP_COLS + j * BANK_TILES * H : gi * GROUP_COLS + (j + 1) * BANK_TILES * H],
-                        op=ALU.mult,
-                    )
-                nc.vector.tensor_tensor(
-                    out=blend_chunk[:, group_cols], in0=gated[:], in1=blend_chunk[:, group_cols], op=ALU.subtract
-                )
-                nc.sync.dma_start(
-                    out=out_rows[:, g * GROUP_COLS : (g + 1) * GROUP_COLS], in_=blend_chunk[:, group_cols]
-                )
+                gated_of[g] = gated
+            s_ps = psum.tile([P, BANK_TILES * H], F32, bufs=4)
+            for i in range(BANK_TILES):
+                n0 = (j * BANK_TILES + i) * P
+                for a in range(HALVES):
+                    block = s_ps[:, i * H + a * P : i * H + (a + 1) * P]
+                    if ((j * BANK_TILES + i) * HALVES + a) % MATMUL_EVERY == 0:
+                        nc.tensor.matmul(
+                            out=block, lhsT=scaled_of[g][:, a, n0 : n0 + P], rhs=ident_f32[:], start=True, stop=True
+                        )
+                    else:
+                        nc.tensor.transpose(block, scaled_of[g][:, a, n0 : n0 + P], ident_f32[:])
+            bank = slice(j * BANK_TILES * H, (j + 1) * BANK_TILES * H)
+            u_bank = slice(gi * GROUP_COLS + j * BANK_TILES * H, gi * GROUP_COLS + (j + 1) * BANK_TILES * H)
+            nc.vector.tensor_tensor(out=gated_of[g][:, bank], in0=s_ps[:], in1=u_sb[c][:, u_bank], op=ALU.mult)
+
+        def finish_rows(g):
+            c, gi = divmod(g, CHUNK_GROUPS)
+            group_cols = slice(gi * GROUP_COLS, (gi + 1) * GROUP_COLS)
+            nc.vector.tensor_tensor(
+                out=blend_sb[c][:, group_cols], in0=gated_of[g][:], in1=blend_sb[c][:, group_cols], op=ALU.subtract
+            )
+            nc.sync.dma_start(out=out_rows[:, g * GROUP_COLS : (g + 1) * GROUP_COLS], in_=blend_sb[c][:, group_cols])
+
+        for c in range(LOAD_BUFS):
+            load_inputs(c)
+        for i in range(-3, GROUPS):
+            if 0 <= i + 1 < GROUPS:
+                multiply(i + 1)
+            if 0 <= i + 2 < GROUPS:
+                quantise(i + 2)
+            for j in range(GROUP_TILES // BANK_TILES):
+                if 0 <= i:
+                    gate_rows(i, j)
+                if i + 3 < GROUPS:
+                    transpose_inputs(i + 3, j)
+            if 0 <= i:
+                finish_rows(i)
+            c, gi = divmod(i + 3, CHUNK_GROUPS)
+            if gi == CHUNK_GROUPS - 1 and c + LOAD_BUFS < CHUNKS:
+                load_inputs(c + LOAD_BUFS)

@@ -5,6 +5,7 @@ from concourse.masks import make_identity
 
 F32 = mybir.dt.float32
 BF16 = mybir.dt.bfloat16
+I32 = mybir.dt.int32
 U32 = mybir.dt.uint32
 U8 = mybir.dt.uint8
 FP8X4 = mybir.dt.float8_e4m3fn_x4
@@ -23,10 +24,9 @@ CHUNK_GROUPS = 2
 CHUNK_COLS = CHUNK_GROUPS * GROUP_COLS
 CHUNKS = ROW_TILES // (GROUP_TILES * CHUNK_GROUPS)
 BANK_TILES = 2
-GROUPS = ROW_TILES // GROUP_TILES
-LOAD_BUFS = 4
 ONES_COLS = 2
 MATMUL_EVERY = 3
+ABS_MASK = 0x7FFF7FFF
 
 FLOPS = 2 * B * (2 * H) * H
 
@@ -53,11 +53,21 @@ def tile_persistentgrucell_pb_t_kernel(
 
     with ExitStack() as ctx:
         const = ctx.enter_context(tc.tile_pool(name="const", bufs=1))
-        keep = ctx.enter_context(tc.tile_pool(name="keep", bufs=1))
-        loads = ctx.enter_context(tc.tile_pool(name="loads", bufs=LOAD_BUFS))
+        h_pool = ctx.enter_context(tc.tile_pool(name="h_pool", bufs=1))
+        loads = ctx.enter_context(tc.tile_pool(name="loads", bufs=5))
+        blend = ctx.enter_context(tc.tile_pool(name="blend", bufs=5))
         work = ctx.enter_context(tc.tile_pool(name="work", bufs=3))
         psum = ctx.enter_context(tc.psum_pool(name="psum", bufs=2))
-        ctx.enter_context(tc.manual_schedule())
+
+        table_warm = const.tile([P, 1], F32)
+        nc.vector.memset(table_warm[:], 0.0)
+        nc.scalar.activation(out=table_warm[:], in_=table_warm[:], func=ACT.Sigmoid)
+        ident_f32 = const.tile([P, P], F32)
+        make_identity(nc, ident_f32[:])
+        ident_bf16 = const.tile([P, P], BF16)
+        make_identity(nc, ident_bf16[:])
+        ones = const.tile([P, ONES_COLS], BF16)
+        nc.vector.memset(ones[:], 1.0)
 
         vec_rows = const.tile([P, P], BF16)
         nc.vector.memset(vec_rows[:], 0.0)
@@ -69,19 +79,34 @@ def tile_persistentgrucell_pb_t_kernel(
         decay_bf16 = const.tile([P, 1], BF16)
         nc.scalar.dma_start(out=decay_bf16[:], in_=connection_decay.partition_broadcast(P))
         w_sb = const.tile([P, HALVES * 2 * H], BF16)
-        nc.sync.dma_start(
+        nc.scalar.dma_start(
             out=w_sb[:].rearrange("p (a k) -> p a k", a=HALVES),
             in_=Wn.rearrange("(a p) k -> p a k", p=P),
         )
-        table_warm = const.tile([P, 1], F32)
-        nc.vector.memset(table_warm[:], 0.0)
-        nc.scalar.activation(out=table_warm[:], in_=table_warm[:], func=ACT.Tanh)
-        ident_f32 = const.tile([P, P], F32)
-        make_identity(nc, ident_f32[:])
-        ident_bf16 = const.tile([P, P], BF16)
-        make_identity(nc, ident_bf16[:])
-        ones = const.tile([P, ONES_COLS], BF16)
-        nc.vector.memset(ones[:], 1.0)
+
+        act_ps = [psum.tile([P, ONES_COLS], F32, tag="m_ps", name="act_ps%d" % a) for a in range(HALVES)]
+        h_sb = []
+        for c in range(CHUNKS):
+            h_chunk = h_pool.tile([P, CHUNK_COLS], BF16, name="h_chunk%d" % c)
+            h_sb.append(h_chunk)
+            nc.sync.dma_start(out=h_chunk[:], in_=h_rows[:, c * CHUNK_COLS : (c + 1) * CHUNK_COLS])
+            h_abs = work.tile([P, CHUNK_COLS], BF16)
+            nc.vector.tensor_scalar(
+                out=h_abs[:].bitcast(I32),
+                in0=h_chunk[:].bitcast(I32),
+                scalar1=ABS_MASK,
+                scalar2=None,
+                op0=ALU.bitwise_and,
+            )
+            blocks = CHUNK_COLS // P
+            for k in range(blocks):
+                nc.tensor.matmul(
+                    out=act_ps[k % HALVES][:],
+                    lhsT=h_abs[:, k * P : (k + 1) * P],
+                    rhs=ones[:],
+                    start=(c == 0 and k < HALVES),
+                    stop=(c == CHUNKS - 1 and k >= blocks - HALVES),
+                )
 
         w_words = w_sb[:].bitcast(F32)
         wt_ps = psum.tile([P, 2, H], F32, tag="xt_ps")
@@ -101,7 +126,7 @@ def tile_persistentgrucell_pb_t_kernel(
         w_scales = const.tile([P, H], U8, align_bytes=64)
         nc.vector.quantize_mx(out=w_codes[:].bitcast(FP8X4), scales=w_scales[:], in_=w_grouped[:])
 
-        vec_ps = psum.tile([P, P], BF16, tag="acc_ps")
+        vec_ps = psum.tile([P, P], BF16, tag="ut_ps")
         nc.tensor.transpose(vec_ps[:], vec_rows[:], ident_bf16[:])
         vec_cols = const.tile([P, 3 * HALVES], F32)
         nc.vector.tensor_copy(out=vec_cols[:], in_=vec_ps[:, 0 : 3 * HALVES])
@@ -110,165 +135,128 @@ def tile_persistentgrucell_pb_t_kernel(
         history_col = vec_cols[:, 2 * HALVES : 3 * HALVES]
         decay_col = const.tile([P, 1], F32)
         nc.vector.tensor_copy(out=decay_col[:], in_=decay_bf16[:])
-        half_decayed = const.tile([P, HALVES], F32)
+        decayed = const.tile([P, HALVES], F32)
         nc.vector.tensor_scalar(
-            out=half_decayed[:], in0=history_col, scalar1=decay_col[:, 0:1], scalar2=0.5, op0=ALU.mult, op1=ALU.mult
+            out=decayed[:], in0=history_col, scalar1=decay_col[:, 0:1], scalar2=None, op0=ALU.mult
         )
-        half_strength = const.tile([P, HALVES], F32)
-        nc.vector.tensor_scalar(out=half_strength[:], in0=strength_col, scalar1=0.5, scalar2=None, op0=ALU.mult)
-
-        act_ps = [psum.tile([P, ONES_COLS], F32, tag="s_ps", bufs=4, name="act_ps%d" % a) for a in range(HALVES)]
-        u_sb = []
-        blend_sb = []
-        for c in range(CHUNKS):
-            chunk_cols = slice(c * CHUNK_COLS, (c + 1) * CHUNK_COLS)
-            h_chunk = keep.tile([P, CHUNK_COLS], BF16, name="h_chunk%d" % c)
-            nc.sync.dma_start(out=h_chunk[:], in_=h_rows[:, chunk_cols])
-            u_chunk = keep.tile([P, CHUNK_COLS], BF16, name="u_chunk%d" % c)
-            u_sb.append(u_chunk)
-            nc.sync.dma_start(out=u_chunk[:], in_=u_rows[:, chunk_cols])
-            h_abs = work.tile([P, CHUNK_COLS], BF16)
-            nc.scalar.activation(out=h_abs[:], in_=h_chunk[:], func=ACT.Abs)
-            blocks = CHUNK_COLS // P
-            for k in range(blocks):
-                nc.tensor.matmul(
-                    out=act_ps[k % HALVES][:],
-                    lhsT=h_abs[:, k * P : (k + 1) * P],
-                    rhs=ones[:],
-                    start=(c == 0 and k < HALVES),
-                    stop=(c == CHUNKS - 1 and k >= blocks - HALVES),
-                )
-            blend_chunk = keep.tile([P, CHUNK_COLS], F32, name="blend_chunk%d" % c)
-            blend_sb.append(blend_chunk)
-            nc.vector.scalar_tensor_tensor(
-                out=blend_chunk[:],
-                in0=u_chunk[:],
-                scalar=1.0,
-                in1=h_chunk[:],
-                op0=ALU.subtract,
-                op1=ALU.mult,
-            )
-
-        tanh_col = const.tile([P, HALVES], F32)
+        gate = const.tile([P, HALVES], F32)
         for a in range(HALVES):
             nc.scalar.activation(
-                out=tanh_col[:, a : a + 1],
+                out=gate[:, a : a + 1],
                 in_=act_ps[a][:, 0:1],
-                func=ACT.Tanh,
-                bias=half_decayed[:, a : a + 1],
-                scale=0.5 / B,
+                func=ACT.Sigmoid,
+                bias=decayed[:, a : a + 1],
+                scale=1.0 / B,
             )
         cs_col = const.tile([P, HALVES], F32)
-        nc.vector.scalar_tensor_tensor(
-            out=cs_col[:], in0=tanh_col[:], scalar=1.0, in1=half_strength[:], op0=ALU.add, op1=ALU.mult
-        )
-        bias_col = const.tile([P, HALVES], F32)
-        nc.vector.tensor_tensor(out=bias_col[:], in0=bn_col, in1=cs_col[:], op=ALU.mult)
+        nc.vector.tensor_tensor(out=cs_col[:], in0=strength_col, in1=gate[:], op=ALU.mult)
 
-        x_words = {}
-        rh_words = {}
-        grouped_of = {}
-        codes_of = {}
-        scales_of = {}
-        scaled_of = {}
-        gated_of = {}
-
-        def load_inputs(c):
+        for c in range(CHUNKS):
             chunk_cols = slice(c * CHUNK_COLS, (c + 1) * CHUNK_COLS)
+            u_chunk = loads.tile([P, CHUNK_COLS], BF16)
+            nc.sync.dma_start(out=u_chunk[:], in_=u_rows[:, chunk_cols])
             x_chunk = loads.tile([P, CHUNK_COLS], BF16)
             nc.sync.dma_start(out=x_chunk[:], in_=x_rows[:, chunk_cols])
             rh_chunk = loads.tile([P, CHUNK_COLS], BF16)
             nc.sync.dma_start(out=rh_chunk[:], in_=rh_rows[:, chunk_cols])
-            x_words[c] = x_chunk[:].bitcast(F32)
-            rh_words[c] = rh_chunk[:].bitcast(F32)
+            x_words = x_chunk[:].bitcast(F32)
+            rh_words = rh_chunk[:].bitcast(F32)
+            kept = blend.tile([P, CHUNK_COLS], F32)
 
-        def transpose_inputs(g, j):
-            c, gi = divmod(g, CHUNK_GROUPS)
-            if j == 0:
+            for gi in range(CHUNK_GROUPS):
+                g = c * CHUNK_GROUPS + gi
+                group_cols = slice(gi * GROUP_COLS, (gi + 1) * GROUP_COLS)
+
+                one_minus_u = work.tile([P, GROUP_COLS], F32)
+                if g % 2 == 0:
+                    nc.scalar.activation(
+                        out=one_minus_u[:], in_=u_chunk[:, group_cols], func=ACT.Copy, bias=1.0, scale=-1.0
+                    )
+                else:
+                    nc.gpsimd.tensor_scalar(
+                        out=one_minus_u[:],
+                        in0=u_chunk[:, group_cols],
+                        scalar1=-1.0,
+                        scalar2=1.0,
+                        op0=ALU.mult,
+                        op1=ALU.add,
+                    )
+                nc.gpsimd.tensor_tensor(
+                    out=kept[:, group_cols], in0=one_minus_u[:], in1=h_sb[c][:, group_cols], op=ALU.mult
+                )
+
                 grouped = work.tile([P, 4 * GROUP_ROWS], BF16, align_bytes=64)
-                grouped_of[g] = grouped
-            grouped_words = grouped_of[g][:].bitcast(F32).rearrange("q (n s) -> q n s", s=2)
-            xt_ps = psum.tile([P, 2, BANK_TILES * P], F32)
-            for i in range(BANK_TILES):
-                t = gi * GROUP_TILES + j * BANK_TILES + i
-                nc.tensor.transpose(xt_ps[:, 0, i * P : (i + 1) * P], x_words[c][:, t * P : (t + 1) * P], ident_f32[:])
-                nc.tensor.transpose(xt_ps[:, 1, i * P : (i + 1) * P], rh_words[c][:, t * P : (t + 1) * P], ident_f32[:])
-            nc.scalar.copy(
-                out=grouped_words[:, j * BANK_TILES * P : (j + 1) * BANK_TILES * P, :],
-                in_=xt_ps[:].rearrange("q s n -> q n s"),
-            )
-
-        def quantise(g):
-            codes = work.tile([P, GROUP_ROWS], U32, align_bytes=64)
-            scales = work.tile([P, GROUP_ROWS], U8, align_bytes=64)
-            nc.vector.quantize_mx(out=codes[:].bitcast(FP8X4), scales=scales[:], in_=grouped_of[g][:])
-            codes_of[g] = codes
-            scales_of[g] = scales
-
-        def multiply(g):
-            scaled = work.tile([P, HALVES, GROUP_ROWS], F32)
-            for a in range(HALVES):
-                acc_ps = psum.tile([P, GROUP_ROWS], F32)
-                nc.tensor.matmul_mx(
-                    out=acc_ps[:],
-                    lhsT=w_codes[:, a * P : (a + 1) * P].bitcast(FP8X4),
-                    lhsT_scale=w_scales[:, a * P : (a + 1) * P],
-                    rhs=codes_of[g][:].bitcast(FP8X4),
-                    rhs_scale=scales_of[g][:],
-                    start=True,
-                    stop=True,
-                )
-                nc.scalar.activation(
-                    out=scaled[:, a, :],
-                    in_=acc_ps[:],
-                    func=ACT.Identity,
-                    bias=bias_col[:, a : a + 1],
-                    scale=cs_col[:, a : a + 1],
-                )
-            scaled_of[g] = scaled
-
-        def gate_rows(g, j):
-            c, gi = divmod(g, CHUNK_GROUPS)
-            if j == 0:
-                gated = work.tile([P, GROUP_COLS], F32)
-                gated_of[g] = gated
-            s_ps = psum.tile([P, BANK_TILES * H], F32, bufs=4)
-            for i in range(BANK_TILES):
-                n0 = (j * BANK_TILES + i) * P
-                for a in range(HALVES):
-                    block = s_ps[:, i * H + a * P : i * H + (a + 1) * P]
-                    if ((j * BANK_TILES + i) * HALVES + a) % MATMUL_EVERY == 0:
-                        nc.tensor.matmul(
-                            out=block, lhsT=scaled_of[g][:, a, n0 : n0 + P], rhs=ident_f32[:], start=True, stop=True
+                grouped_words = grouped[:].bitcast(F32).rearrange("q (n s) -> q n s", s=2)
+                for j in range(GROUP_TILES // BANK_TILES):
+                    xt_ps = psum.tile([P, 2, BANK_TILES * P], F32)
+                    for i in range(BANK_TILES):
+                        t = gi * GROUP_TILES + j * BANK_TILES + i
+                        nc.tensor.transpose(
+                            xt_ps[:, 0, i * P : (i + 1) * P], x_words[:, t * P : (t + 1) * P], ident_f32[:]
                         )
-                    else:
-                        nc.tensor.transpose(block, scaled_of[g][:, a, n0 : n0 + P], ident_f32[:])
-            bank = slice(j * BANK_TILES * H, (j + 1) * BANK_TILES * H)
-            u_bank = slice(gi * GROUP_COLS + j * BANK_TILES * H, gi * GROUP_COLS + (j + 1) * BANK_TILES * H)
-            nc.vector.tensor_tensor(out=gated_of[g][:, bank], in0=s_ps[:], in1=u_sb[c][:, u_bank], op=ALU.mult)
+                        nc.tensor.transpose(
+                            xt_ps[:, 1, i * P : (i + 1) * P], rh_words[:, t * P : (t + 1) * P], ident_f32[:]
+                        )
+                    nc.scalar.copy(
+                        out=grouped_words[:, j * BANK_TILES * P : (j + 1) * BANK_TILES * P, :],
+                        in_=xt_ps[:].rearrange("q s n -> q n s"),
+                    )
+                codes = work.tile([P, GROUP_ROWS], U32, align_bytes=64)
+                scales = work.tile([P, GROUP_ROWS], U8, align_bytes=64)
+                nc.vector.quantize_mx(out=codes[:].bitcast(FP8X4), scales=scales[:], in_=grouped[:])
 
-        def finish_rows(g):
-            c, gi = divmod(g, CHUNK_GROUPS)
-            group_cols = slice(gi * GROUP_COLS, (gi + 1) * GROUP_COLS)
-            nc.vector.tensor_tensor(
-                out=blend_sb[c][:, group_cols], in0=gated_of[g][:], in1=blend_sb[c][:, group_cols], op=ALU.subtract
-            )
-            nc.sync.dma_start(out=out_rows[:, g * GROUP_COLS : (g + 1) * GROUP_COLS], in_=blend_sb[c][:, group_cols])
+                ut_ps = psum.tile([P, HALVES, GROUP_ROWS], BF16)
+                for i in range(GROUP_TILES):
+                    for a in range(HALVES):
+                        col = (gi * GROUP_TILES + i) * H + a * P
+                        nc.tensor.transpose(
+                            ut_ps[:, a, i * P : (i + 1) * P], u_chunk[:, col : col + P], ident_bf16[:]
+                        )
+                u_cs = work.tile([P, HALVES, GROUP_ROWS], F32)
+                for a in range(HALVES):
+                    nc.scalar.activation(
+                        out=u_cs[:, a, :], in_=ut_ps[:, a, :], func=ACT.Copy, scale=cs_col[:, a : a + 1]
+                    )
 
-        for c in range(LOAD_BUFS):
-            load_inputs(c)
-        for i in range(-3, GROUPS):
-            if 0 <= i + 1 < GROUPS:
-                multiply(i + 1)
-            if 0 <= i + 2 < GROUPS:
-                quantise(i + 2)
-            for j in range(GROUP_TILES // BANK_TILES):
-                if 0 <= i:
-                    gate_rows(i, j)
-                if i + 3 < GROUPS:
-                    transpose_inputs(i + 3, j)
-            if 0 <= i:
-                finish_rows(i)
-            c, gi = divmod(i + 3, CHUNK_GROUPS)
-            if gi == CHUNK_GROUPS - 1 and c + LOAD_BUFS < CHUNKS:
-                load_inputs(c + LOAD_BUFS)
+                gated = work.tile([P, HALVES, GROUP_ROWS], F32)
+                for a in range(HALVES):
+                    acc_ps = psum.tile([P, GROUP_ROWS], F32)
+                    nc.tensor.matmul_mx(
+                        out=acc_ps[:],
+                        lhsT=w_codes[:, a * P : (a + 1) * P].bitcast(FP8X4),
+                        lhsT_scale=w_scales[:, a * P : (a + 1) * P],
+                        rhs=codes[:].bitcast(FP8X4),
+                        rhs_scale=scales[:],
+                        start=True,
+                        stop=True,
+                    )
+                    nc.vector.scalar_tensor_tensor(
+                        out=gated[:, a, :],
+                        in0=acc_ps[:],
+                        scalar=bn_col[:, a : a + 1],
+                        in1=u_cs[:, a, :],
+                        op0=ALU.add,
+                        op1=ALU.mult,
+                    )
+
+                for j in range(GROUP_TILES // BANK_TILES):
+                    m_ps = psum.tile([P, BANK_TILES * H], F32)
+                    for i in range(BANK_TILES):
+                        n0 = (j * BANK_TILES + i) * P
+                        for a in range(HALVES):
+                            block = m_ps[:, i * H + a * P : i * H + (a + 1) * P]
+                            if ((j * BANK_TILES + i) * HALVES + a) % MATMUL_EVERY == 0:
+                                nc.tensor.matmul(
+                                    out=block, lhsT=gated[:, a, n0 : n0 + P], rhs=ident_f32[:], start=True, stop=True
+                                )
+                            else:
+                                nc.tensor.transpose(block, gated[:, a, n0 : n0 + P], ident_f32[:])
+                    bank_cols = slice(
+                        gi * GROUP_COLS + j * BANK_TILES * H, gi * GROUP_COLS + (j + 1) * BANK_TILES * H
+                    )
+                    nc.vector.tensor_tensor(
+                        out=kept[:, bank_cols], in0=m_ps[:], in1=kept[:, bank_cols], op=ALU.add
+                    )
+                nc.sync.dma_start(
+                    out=out_rows[:, g * GROUP_COLS : (g + 1) * GROUP_COLS], in_=kept[:, group_cols]
+                )

@@ -5,7 +5,6 @@ from concourse.masks import make_identity
 
 F32 = mybir.dt.float32
 BF16 = mybir.dt.bfloat16
-I32 = mybir.dt.int32
 U32 = mybir.dt.uint32
 U8 = mybir.dt.uint8
 FP8X4 = mybir.dt.float8_e4m3fn_x4
@@ -24,9 +23,11 @@ CHUNK_GROUPS = 2
 CHUNK_COLS = CHUNK_GROUPS * GROUP_COLS
 CHUNKS = ROW_TILES // (GROUP_TILES * CHUNK_GROUPS)
 BANK_TILES = 2
+GROUPS = ROW_TILES // GROUP_TILES
+LOAD_BUFS = 4
 ONES_COLS = 2
+GPSIMD_TILES = 1
 MATMUL_EVERY = 3
-ABS_MASK = 0x7FFF7FFF
 
 FLOPS = 2 * B * (2 * H) * H
 
@@ -53,21 +54,11 @@ def tile_persistentgrucell_pb_t_kernel(
 
     with ExitStack() as ctx:
         const = ctx.enter_context(tc.tile_pool(name="const", bufs=1))
-        h_pool = ctx.enter_context(tc.tile_pool(name="h_pool", bufs=1))
-        loads = ctx.enter_context(tc.tile_pool(name="loads", bufs=5))
-        blend = ctx.enter_context(tc.tile_pool(name="blend", bufs=5))
+        keep = ctx.enter_context(tc.tile_pool(name="keep", bufs=1))
+        loads = ctx.enter_context(tc.tile_pool(name="loads", bufs=LOAD_BUFS))
         work = ctx.enter_context(tc.tile_pool(name="work", bufs=3))
         psum = ctx.enter_context(tc.psum_pool(name="psum", bufs=2))
-
-        table_warm = const.tile([P, 1], F32)
-        nc.vector.memset(table_warm[:], 0.0)
-        nc.scalar.activation(out=table_warm[:], in_=table_warm[:], func=ACT.Sigmoid)
-        ident_f32 = const.tile([P, P], F32)
-        make_identity(nc, ident_f32[:])
-        ident_bf16 = const.tile([P, P], BF16)
-        make_identity(nc, ident_bf16[:])
-        ones = const.tile([P, ONES_COLS], BF16)
-        nc.vector.memset(ones[:], 1.0)
+        ctx.enter_context(tc.manual_schedule())
 
         vec_rows = const.tile([P, P], BF16)
         nc.vector.memset(vec_rows[:], 0.0)
@@ -79,34 +70,19 @@ def tile_persistentgrucell_pb_t_kernel(
         decay_bf16 = const.tile([P, 1], BF16)
         nc.scalar.dma_start(out=decay_bf16[:], in_=connection_decay.partition_broadcast(P))
         w_sb = const.tile([P, HALVES * 2 * H], BF16)
-        nc.scalar.dma_start(
+        nc.sync.dma_start(
             out=w_sb[:].rearrange("p (a k) -> p a k", a=HALVES),
             in_=Wn.rearrange("(a p) k -> p a k", p=P),
         )
-
-        act_ps = [psum.tile([P, ONES_COLS], F32, tag="m_ps", name="act_ps%d" % a) for a in range(HALVES)]
-        h_sb = []
-        for c in range(CHUNKS):
-            h_chunk = h_pool.tile([P, CHUNK_COLS], BF16, name="h_chunk%d" % c)
-            h_sb.append(h_chunk)
-            nc.sync.dma_start(out=h_chunk[:], in_=h_rows[:, c * CHUNK_COLS : (c + 1) * CHUNK_COLS])
-            h_abs = work.tile([P, CHUNK_COLS], BF16)
-            nc.vector.tensor_scalar(
-                out=h_abs[:].bitcast(I32),
-                in0=h_chunk[:].bitcast(I32),
-                scalar1=ABS_MASK,
-                scalar2=None,
-                op0=ALU.bitwise_and,
-            )
-            blocks = CHUNK_COLS // P
-            for k in range(blocks):
-                nc.tensor.matmul(
-                    out=act_ps[k % HALVES][:],
-                    lhsT=h_abs[:, k * P : (k + 1) * P],
-                    rhs=ones[:],
-                    start=(c == 0 and k < HALVES),
-                    stop=(c == CHUNKS - 1 and k >= blocks - HALVES),
-                )
+        table_warm = const.tile([P, 1], F32)
+        nc.vector.memset(table_warm[:], 0.0)
+        nc.scalar.activation(out=table_warm[:], in_=table_warm[:], func=ACT.Tanh)
+        ident_f32 = const.tile([P, P], F32)
+        make_identity(nc, ident_f32[:])
+        ident_bf16 = const.tile([P, P], BF16)
+        make_identity(nc, ident_bf16[:])
+        ones = const.tile([P, ONES_COLS], BF16)
+        nc.vector.memset(ones[:], 1.0)
 
         w_words = w_sb[:].bitcast(F32)
         wt_ps = psum.tile([P, 2, H], F32, tag="xt_ps")
@@ -126,7 +102,7 @@ def tile_persistentgrucell_pb_t_kernel(
         w_scales = const.tile([P, H], U8, align_bytes=64)
         nc.vector.quantize_mx(out=w_codes[:].bitcast(FP8X4), scales=w_scales[:], in_=w_grouped[:])
 
-        vec_ps = psum.tile([P, P], BF16, tag="ut_ps")
+        vec_ps = psum.tile([P, P], BF16, tag="acc_ps")
         nc.tensor.transpose(vec_ps[:], vec_rows[:], ident_bf16[:])
         vec_cols = const.tile([P, 3 * HALVES], F32)
         nc.vector.tensor_copy(out=vec_cols[:], in_=vec_ps[:, 0 : 3 * HALVES])
@@ -135,128 +111,168 @@ def tile_persistentgrucell_pb_t_kernel(
         history_col = vec_cols[:, 2 * HALVES : 3 * HALVES]
         decay_col = const.tile([P, 1], F32)
         nc.vector.tensor_copy(out=decay_col[:], in_=decay_bf16[:])
-        decayed = const.tile([P, HALVES], F32)
+        half_decayed = const.tile([P, HALVES], F32)
         nc.vector.tensor_scalar(
-            out=decayed[:], in0=history_col, scalar1=decay_col[:, 0:1], scalar2=None, op0=ALU.mult
+            out=half_decayed[:], in0=history_col, scalar1=decay_col[:, 0:1], scalar2=0.5, op0=ALU.mult, op1=ALU.mult
         )
-        gate = const.tile([P, HALVES], F32)
-        for a in range(HALVES):
-            nc.scalar.activation(
-                out=gate[:, a : a + 1],
-                in_=act_ps[a][:, 0:1],
-                func=ACT.Sigmoid,
-                bias=decayed[:, a : a + 1],
-                scale=1.0 / B,
-            )
-        cs_col = const.tile([P, HALVES], F32)
-        nc.vector.tensor_tensor(out=cs_col[:], in0=strength_col, in1=gate[:], op=ALU.mult)
+        half_strength = const.tile([P, HALVES], F32)
+        nc.vector.tensor_scalar(out=half_strength[:], in0=strength_col, scalar1=0.5, scalar2=None, op0=ALU.mult)
 
+        act_ps = [psum.tile([P, ONES_COLS], F32, tag="s_ps", bufs=4, name="act_ps%d" % a) for a in range(HALVES)]
+        u_sb = []
+        blend_sb = []
         for c in range(CHUNKS):
             chunk_cols = slice(c * CHUNK_COLS, (c + 1) * CHUNK_COLS)
-            u_chunk = loads.tile([P, CHUNK_COLS], BF16)
+            h_chunk = keep.tile([P, CHUNK_COLS], BF16, name="h_chunk%d" % c)
+            nc.sync.dma_start(out=h_chunk[:], in_=h_rows[:, chunk_cols])
+            u_chunk = keep.tile([P, CHUNK_COLS], BF16, name="u_chunk%d" % c)
+            u_sb.append(u_chunk)
             nc.sync.dma_start(out=u_chunk[:], in_=u_rows[:, chunk_cols])
+            h_abs = work.tile([P, CHUNK_COLS], BF16)
+            nc.scalar.activation(out=h_abs[:], in_=h_chunk[:], func=ACT.Abs)
+            blocks = CHUNK_COLS // P
+            for k in range(blocks):
+                nc.tensor.matmul(
+                    out=act_ps[k % HALVES][:],
+                    lhsT=h_abs[:, k * P : (k + 1) * P],
+                    rhs=ones[:],
+                    start=(c == 0 and k < HALVES),
+                    stop=(c == CHUNKS - 1 and k >= blocks - HALVES),
+                )
+            blend_chunk = keep.tile([P, CHUNK_COLS], F32, name="blend_chunk%d" % c)
+            blend_sb.append(blend_chunk)
+            nc.vector.scalar_tensor_tensor(
+                out=blend_chunk[:],
+                in0=u_chunk[:],
+                scalar=1.0,
+                in1=h_chunk[:],
+                op0=ALU.subtract,
+                op1=ALU.mult,
+            )
+
+        tanh_col = const.tile([P, HALVES], F32)
+        for a in range(HALVES):
+            nc.scalar.activation(
+                out=tanh_col[:, a : a + 1],
+                in_=act_ps[a][:, 0:1],
+                func=ACT.Tanh,
+                bias=half_decayed[:, a : a + 1],
+                scale=0.5 / B,
+            )
+        cs_col = const.tile([P, HALVES], F32)
+        nc.vector.scalar_tensor_tensor(
+            out=cs_col[:], in0=tanh_col[:], scalar=1.0, in1=half_strength[:], op0=ALU.add, op1=ALU.mult
+        )
+        bias_col = const.tile([P, HALVES], F32)
+        nc.vector.tensor_tensor(out=bias_col[:], in0=bn_col, in1=cs_col[:], op=ALU.mult)
+
+        x_words = {}
+        rh_words = {}
+        grouped_of = {}
+        codes_of = {}
+        scales_of = {}
+        scaled_of = {}
+        gated_of = {}
+
+        def load_inputs(c):
+            chunk_cols = slice(c * CHUNK_COLS, (c + 1) * CHUNK_COLS)
             x_chunk = loads.tile([P, CHUNK_COLS], BF16)
             nc.sync.dma_start(out=x_chunk[:], in_=x_rows[:, chunk_cols])
             rh_chunk = loads.tile([P, CHUNK_COLS], BF16)
             nc.sync.dma_start(out=rh_chunk[:], in_=rh_rows[:, chunk_cols])
-            x_words = x_chunk[:].bitcast(F32)
-            rh_words = rh_chunk[:].bitcast(F32)
-            kept = blend.tile([P, CHUNK_COLS], F32)
+            x_words[c] = x_chunk[:].bitcast(F32)
+            rh_words[c] = rh_chunk[:].bitcast(F32)
 
-            for gi in range(CHUNK_GROUPS):
-                g = c * CHUNK_GROUPS + gi
-                group_cols = slice(gi * GROUP_COLS, (gi + 1) * GROUP_COLS)
-
-                one_minus_u = work.tile([P, GROUP_COLS], F32)
-                if g % 2 == 0:
-                    nc.scalar.activation(
-                        out=one_minus_u[:], in_=u_chunk[:, group_cols], func=ACT.Copy, bias=1.0, scale=-1.0
-                    )
-                else:
-                    nc.gpsimd.tensor_scalar(
-                        out=one_minus_u[:],
-                        in0=u_chunk[:, group_cols],
-                        scalar1=-1.0,
-                        scalar2=1.0,
-                        op0=ALU.mult,
-                        op1=ALU.add,
-                    )
-                nc.gpsimd.tensor_tensor(
-                    out=kept[:, group_cols], in0=one_minus_u[:], in1=h_sb[c][:, group_cols], op=ALU.mult
-                )
-
+        def transpose_inputs(g, j):
+            c, gi = divmod(g, CHUNK_GROUPS)
+            if j == 0:
                 grouped = work.tile([P, 4 * GROUP_ROWS], BF16, align_bytes=64)
-                grouped_words = grouped[:].bitcast(F32).rearrange("q (n s) -> q n s", s=2)
-                for j in range(GROUP_TILES // BANK_TILES):
-                    xt_ps = psum.tile([P, 2, BANK_TILES * P], F32)
-                    for i in range(BANK_TILES):
-                        t = gi * GROUP_TILES + j * BANK_TILES + i
-                        nc.tensor.transpose(
-                            xt_ps[:, 0, i * P : (i + 1) * P], x_words[:, t * P : (t + 1) * P], ident_f32[:]
-                        )
-                        nc.tensor.transpose(
-                            xt_ps[:, 1, i * P : (i + 1) * P], rh_words[:, t * P : (t + 1) * P], ident_f32[:]
-                        )
-                    nc.scalar.copy(
-                        out=grouped_words[:, j * BANK_TILES * P : (j + 1) * BANK_TILES * P, :],
-                        in_=xt_ps[:].rearrange("q s n -> q n s"),
-                    )
-                codes = work.tile([P, GROUP_ROWS], U32, align_bytes=64)
-                scales = work.tile([P, GROUP_ROWS], U8, align_bytes=64)
-                nc.vector.quantize_mx(out=codes[:].bitcast(FP8X4), scales=scales[:], in_=grouped[:])
+                grouped_of[g] = grouped
+            grouped_words = grouped_of[g][:].bitcast(F32).rearrange("q (n s) -> q n s", s=2)
+            xt_ps = psum.tile([P, 2, BANK_TILES * P], F32)
+            for i in range(BANK_TILES):
+                t = gi * GROUP_TILES + j * BANK_TILES + i
+                nc.tensor.transpose(xt_ps[:, 0, i * P : (i + 1) * P], x_words[c][:, t * P : (t + 1) * P], ident_f32[:])
+                nc.tensor.transpose(xt_ps[:, 1, i * P : (i + 1) * P], rh_words[c][:, t * P : (t + 1) * P], ident_f32[:])
+            nc.scalar.copy(
+                out=grouped_words[:, j * BANK_TILES * P : (j + 1) * BANK_TILES * P, :],
+                in_=xt_ps[:].rearrange("q s n -> q n s"),
+            )
 
-                ut_ps = psum.tile([P, HALVES, GROUP_ROWS], BF16)
-                for i in range(GROUP_TILES):
-                    for a in range(HALVES):
-                        col = (gi * GROUP_TILES + i) * H + a * P
-                        nc.tensor.transpose(
-                            ut_ps[:, a, i * P : (i + 1) * P], u_chunk[:, col : col + P], ident_bf16[:]
-                        )
-                u_cs = work.tile([P, HALVES, GROUP_ROWS], F32)
-                for a in range(HALVES):
-                    nc.scalar.activation(
-                        out=u_cs[:, a, :], in_=ut_ps[:, a, :], func=ACT.Copy, scale=cs_col[:, a : a + 1]
-                    )
+        def quantise(g):
+            codes = work.tile([P, GROUP_ROWS], U32, align_bytes=64)
+            scales = work.tile([P, GROUP_ROWS], U8, align_bytes=64)
+            nc.vector.quantize_mx(out=codes[:].bitcast(FP8X4), scales=scales[:], in_=grouped_of[g][:])
+            codes_of[g] = codes
+            scales_of[g] = scales
 
-                gated = work.tile([P, HALVES, GROUP_ROWS], F32)
-                for a in range(HALVES):
-                    acc_ps = psum.tile([P, GROUP_ROWS], F32)
-                    nc.tensor.matmul_mx(
-                        out=acc_ps[:],
-                        lhsT=w_codes[:, a * P : (a + 1) * P].bitcast(FP8X4),
-                        lhsT_scale=w_scales[:, a * P : (a + 1) * P],
-                        rhs=codes[:].bitcast(FP8X4),
-                        rhs_scale=scales[:],
-                        start=True,
-                        stop=True,
-                    )
-                    nc.vector.scalar_tensor_tensor(
-                        out=gated[:, a, :],
-                        in0=acc_ps[:],
-                        scalar=bn_col[:, a : a + 1],
-                        in1=u_cs[:, a, :],
-                        op0=ALU.add,
-                        op1=ALU.mult,
-                    )
-
-                for j in range(GROUP_TILES // BANK_TILES):
-                    m_ps = psum.tile([P, BANK_TILES * H], F32)
-                    for i in range(BANK_TILES):
-                        n0 = (j * BANK_TILES + i) * P
-                        for a in range(HALVES):
-                            block = m_ps[:, i * H + a * P : i * H + (a + 1) * P]
-                            if ((j * BANK_TILES + i) * HALVES + a) % MATMUL_EVERY == 0:
-                                nc.tensor.matmul(
-                                    out=block, lhsT=gated[:, a, n0 : n0 + P], rhs=ident_f32[:], start=True, stop=True
-                                )
-                            else:
-                                nc.tensor.transpose(block, gated[:, a, n0 : n0 + P], ident_f32[:])
-                    bank_cols = slice(
-                        gi * GROUP_COLS + j * BANK_TILES * H, gi * GROUP_COLS + (j + 1) * BANK_TILES * H
-                    )
-                    nc.vector.tensor_tensor(
-                        out=kept[:, bank_cols], in0=m_ps[:], in1=kept[:, bank_cols], op=ALU.add
-                    )
-                nc.sync.dma_start(
-                    out=out_rows[:, g * GROUP_COLS : (g + 1) * GROUP_COLS], in_=kept[:, group_cols]
+        def multiply(g):
+            scaled = work.tile([P, HALVES, GROUP_ROWS], F32)
+            for a in range(HALVES):
+                acc_ps = psum.tile([P, GROUP_ROWS], F32)
+                nc.tensor.matmul_mx(
+                    out=acc_ps[:],
+                    lhsT=w_codes[:, a * P : (a + 1) * P].bitcast(FP8X4),
+                    lhsT_scale=w_scales[:, a * P : (a + 1) * P],
+                    rhs=codes_of[g][:].bitcast(FP8X4),
+                    rhs_scale=scales_of[g][:],
+                    start=True,
+                    stop=True,
                 )
+                nc.scalar.activation(
+                    out=scaled[:, a, :],
+                    in_=acc_ps[:],
+                    func=ACT.Identity,
+                    bias=bias_col[:, a : a + 1],
+                    scale=cs_col[:, a : a + 1],
+                )
+            scaled_of[g] = scaled
+
+        def gate_rows(g, j):
+            c, gi = divmod(g, CHUNK_GROUPS)
+            if j == 0:
+                gated = work.tile([P, GROUP_COLS], F32)
+                gated_of[g] = gated
+            s_ps = psum.tile([P, BANK_TILES * H], F32, bufs=4)
+            for i in range(BANK_TILES):
+                n0 = (j * BANK_TILES + i) * P
+                for a in range(HALVES):
+                    block = s_ps[:, i * H + a * P : i * H + (a + 1) * P]
+                    if ((j * BANK_TILES + i) * HALVES + a) % MATMUL_EVERY == 0:
+                        nc.tensor.matmul(
+                            out=block, lhsT=scaled_of[g][:, a, n0 : n0 + P], rhs=ident_f32[:], start=True, stop=True
+                        )
+                    else:
+                        nc.tensor.transpose(block, scaled_of[g][:, a, n0 : n0 + P], ident_f32[:])
+            bank = slice(j * BANK_TILES * H, (j + 1) * BANK_TILES * H)
+            u_bank = slice(gi * GROUP_COLS + j * BANK_TILES * H, gi * GROUP_COLS + (j + 1) * BANK_TILES * H)
+            nc.vector.tensor_tensor(out=gated_of[g][:, bank], in0=s_ps[:], in1=u_sb[c][:, u_bank], op=ALU.mult)
+
+        def finish_rows(g):
+            c, gi = divmod(g, CHUNK_GROUPS)
+            group_cols = slice(gi * GROUP_COLS, (gi + 1) * GROUP_COLS)
+            split = GROUP_COLS - GPSIMD_TILES * H
+            for engine, lo, hi in ((nc.vector, 0, split), (nc.gpsimd, split, GROUP_COLS)):
+                cols = slice(gi * GROUP_COLS + lo, gi * GROUP_COLS + hi)
+                engine.tensor_tensor(
+                    out=blend_sb[c][:, cols], in0=gated_of[g][:, lo:hi], in1=blend_sb[c][:, cols], op=ALU.subtract
+                )
+            nc.sync.dma_start(out=out_rows[:, g * GROUP_COLS : (g + 1) * GROUP_COLS], in_=blend_sb[c][:, group_cols])
+
+        for c in range(LOAD_BUFS):
+            load_inputs(c)
+        for i in range(-3, GROUPS):
+            if 0 <= i + 1 < GROUPS:
+                multiply(i + 1)
+            if 0 <= i + 2 < GROUPS:
+                quantise(i + 2)
+            for j in range(GROUP_TILES // BANK_TILES):
+                if 0 <= i:
+                    gate_rows(i, j)
+                if i + 3 < GROUPS:
+                    transpose_inputs(i + 3, j)
+            if 0 <= i:
+                finish_rows(i)
+            c, gi = divmod(i + 3, CHUNK_GROUPS)
+            if gi == CHUNK_GROUPS - 1 and c + LOAD_BUFS < CHUNKS:
+                load_inputs(c + LOAD_BUFS)

@@ -26,7 +26,7 @@ BANK_TILES = 2
 GROUPS = ROW_TILES // GROUP_TILES
 LOAD_BUFS = 4
 ONES_COLS = 2
-GPSIMD_TILES = 1
+GPSIMD_TILES = 2
 MATMUL_EVERY = 3
 
 FLOPS = 2 * B * (2 * H) * H

@@ -27,7 +27,7 @@ GROUPS = ROW_TILES // GROUP_TILES
 LOAD_BUFS = 4
 ONES_COLS = 2
 GPSIMD_TILES = 2
-MATMUL_EVERY = 3
+MATMUL_EVERY = 4
 
 FLOPS = 2 * B * (2 * H) * H
 

from contextlib import ExitStack

import concourse.mybir as mybir
from concourse.masks import make_identity

F32 = mybir.dt.float32
BF16 = mybir.dt.bfloat16
U32 = mybir.dt.uint32
U8 = mybir.dt.uint8
FP8X4 = mybir.dt.float8_e4m3fn_x4
ALU = mybir.AluOpType
ACT = mybir.ActivationFunctionType

P = 128
B = 8192
H = 256
HALVES = H // P
ROW_TILES = B // P
GROUP_TILES = 4
GROUP_ROWS = GROUP_TILES * P
GROUP_COLS = GROUP_TILES * H
CHUNK_GROUPS = 2
CHUNK_COLS = CHUNK_GROUPS * GROUP_COLS
CHUNKS = ROW_TILES // (GROUP_TILES * CHUNK_GROUPS)
BANK_TILES = 2
GROUPS = ROW_TILES // GROUP_TILES
LOAD_BUFS = 4
ONES_COLS = 2
GPSIMD_TILES = 2
MATMUL_EVERY = 4

FLOPS = 2 * B * (2 * H) * H


def tile_persistentgrucell_pb_t_kernel(
    tc,
    x,
    rh,
    update,
    hidden,
    Wn,
    bn,
    connection_strength,
    connection_decay,
    connection_history,
    out,
):
    nc = tc.nc
    x_rows = x.rearrange("(p t) k -> p (t k)", t=ROW_TILES)
    rh_rows = rh.rearrange("(p t) k -> p (t k)", t=ROW_TILES)
    u_rows = update.rearrange("(p t) k -> p (t k)", t=ROW_TILES)
    h_rows = hidden.rearrange("(p t) k -> p (t k)", t=ROW_TILES)
    out_rows = out.rearrange("(p t) k -> p (t k)", t=ROW_TILES)

    with ExitStack() as ctx:
        const = ctx.enter_context(tc.tile_pool(name="const", bufs=1))
        keep = ctx.enter_context(tc.tile_pool(name="keep", bufs=1))
        loads = ctx.enter_context(tc.tile_pool(name="loads", bufs=LOAD_BUFS))
        work = ctx.enter_context(tc.tile_pool(name="work", bufs=3))
        psum = ctx.enter_context(tc.psum_pool(name="psum", bufs=2))
        ctx.enter_context(tc.manual_schedule())

        vec_rows = const.tile([P, P], BF16)
        nc.vector.memset(vec_rows[:], 0.0)
        for r, vec in enumerate((bn, connection_strength, connection_history)):
            nc.scalar.dma_start(
                out=vec_rows[HALVES * r : HALVES * (r + 1), :],
                in_=vec.rearrange("(a c) -> a c", a=HALVES),
            )
        decay_bf16 = const.tile([P, 1], BF16)
        nc.scalar.dma_start(out=decay_bf16[:], in_=connection_decay.partition_broadcast(P))
        w_sb = const.tile([P, HALVES * 2 * H], BF16)
        nc.sync.dma_start(
            out=w_sb[:].rearrange("p (a k) -> p a k", a=HALVES),
            in_=Wn.rearrange("(a p) k -> p a k", p=P),
        )
        table_warm = const.tile([P, 1], F32)
        nc.vector.memset(table_warm[:], 0.0)
        nc.scalar.activation(out=table_warm[:], in_=table_warm[:], func=ACT.Tanh)
        ident_f32 = const.tile([P, P], F32)
        make_identity(nc, ident_f32[:])
        ident_bf16 = const.tile([P, P], BF16)
        make_identity(nc, ident_bf16[:])
        ones = const.tile([P, ONES_COLS], BF16)
        nc.vector.memset(ones[:], 1.0)

        w_words = w_sb[:].bitcast(F32)
        wt_ps = psum.tile([P, 2, H], F32, tag="xt_ps")
        for a in range(HALVES):
            for s in range(2):
                nc.tensor.transpose(
                    wt_ps[:, s, a * P : (a + 1) * P],
                    w_words[:, (a * 2 + s) * P : (a * 2 + s + 1) * P],
                    ident_f32[:],
                )
        w_grouped = const.tile([P, 4 * H], BF16, align_bytes=64)
        nc.vector.tensor_copy(
            out=w_grouped[:].bitcast(F32).rearrange("q (n s) -> q n s", s=2),
            in_=wt_ps[:].rearrange("q s n -> q n s"),
        )
        w_codes = const.tile([P, H], U32, align_bytes=64)
        w_scales = const.tile([P, H], U8, align_bytes=64)
        nc.vector.quantize_mx(out=w_codes[:].bitcast(FP8X4), scales=w_scales[:], in_=w_grouped[:])

        vec_ps = psum.tile([P, P], BF16, tag="acc_ps")
        nc.tensor.transpose(vec_ps[:], vec_rows[:], ident_bf16[:])
        vec_cols = const.tile([P, 3 * HALVES], F32)
        nc.vector.tensor_copy(out=vec_cols[:], in_=vec_ps[:, 0 : 3 * HALVES])
        bn_col = vec_cols[:, 0:HALVES]
        strength_col = vec_cols[:, HALVES : 2 * HALVES]
        history_col = vec_cols[:, 2 * HALVES : 3 * HALVES]
        decay_col = const.tile([P, 1], F32)
        nc.vector.tensor_copy(out=decay_col[:], in_=decay_bf16[:])
        half_decayed = const.tile([P, HALVES], F32)
        nc.vector.tensor_scalar(
            out=half_decayed[:], in0=history_col, scalar1=decay_col[:, 0:1], scalar2=0.5, op0=ALU.mult, op1=ALU.mult
        )
        half_strength = const.tile([P, HALVES], F32)
        nc.vector.tensor_scalar(out=half_strength[:], in0=strength_col, scalar1=0.5, scalar2=None, op0=ALU.mult)

        act_ps = [psum.tile([P, ONES_COLS], F32, tag="s_ps", bufs=4, name="act_ps%d" % a) for a in range(HALVES)]
        u_sb = []
        blend_sb = []
        for c in range(CHUNKS):
            chunk_cols = slice(c * CHUNK_COLS, (c + 1) * CHUNK_COLS)
            h_chunk = keep.tile([P, CHUNK_COLS], BF16, name="h_chunk%d" % c)
            nc.sync.dma_start(out=h_chunk[:], in_=h_rows[:, chunk_cols])
            u_chunk = keep.tile([P, CHUNK_COLS], BF16, name="u_chunk%d" % c)
            u_sb.append(u_chunk)
            nc.sync.dma_start(out=u_chunk[:], in_=u_rows[:, chunk_cols])
            h_abs = work.tile([P, CHUNK_COLS], BF16)
            nc.scalar.activation(out=h_abs[:], in_=h_chunk[:], func=ACT.Abs)
            blocks = CHUNK_COLS // P
            for k in range(blocks):
                nc.tensor.matmul(
                    out=act_ps[k % HALVES][:],
                    lhsT=h_abs[:, k * P : (k + 1) * P],
                    rhs=ones[:],
                    start=(c == 0 and k < HALVES),
                    stop=(c == CHUNKS - 1 and k >= blocks - HALVES),
                )
            blend_chunk = keep.tile([P, CHUNK_COLS], F32, name="blend_chunk%d" % c)
            blend_sb.append(blend_chunk)
            nc.vector.scalar_tensor_tensor(
                out=blend_chunk[:],
                in0=u_chunk[:],
                scalar=1.0,
                in1=h_chunk[:],
                op0=ALU.subtract,
                op1=ALU.mult,
            )

        tanh_col = const.tile([P, HALVES], F32)
        for a in range(HALVES):
            nc.scalar.activation(
                out=tanh_col[:, a : a + 1],
                in_=act_ps[a][:, 0:1],
                func=ACT.Tanh,
                bias=half_decayed[:, a : a + 1],
                scale=0.5 / B,
            )
        cs_col = const.tile([P, HALVES], F32)
        nc.vector.scalar_tensor_tensor(
            out=cs_col[:], in0=tanh_col[:], scalar=1.0, in1=half_strength[:], op0=ALU.add, op1=ALU.mult
        )
        bias_col = const.tile([P, HALVES], F32)
        nc.vector.tensor_tensor(out=bias_col[:], in0=bn_col, in1=cs_col[:], op=ALU.mult)

        x_words = {}
        rh_words = {}
        grouped_of = {}
        codes_of = {}
        scales_of = {}
        scaled_of = {}
        gated_of = {}

        def load_inputs(c):
            chunk_cols = slice(c * CHUNK_COLS, (c + 1) * CHUNK_COLS)
            x_chunk = loads.tile([P, CHUNK_COLS], BF16)
            nc.sync.dma_start(out=x_chunk[:], in_=x_rows[:, chunk_cols])
            rh_chunk = loads.tile([P, CHUNK_COLS], BF16)
            nc.sync.dma_start(out=rh_chunk[:], in_=rh_rows[:, chunk_cols])
            x_words[c] = x_chunk[:].bitcast(F32)
            rh_words[c] = rh_chunk[:].bitcast(F32)

        def transpose_inputs(g, j):
            c, gi = divmod(g, CHUNK_GROUPS)
            if j == 0:
                grouped = work.tile([P, 4 * GROUP_ROWS], BF16, align_bytes=64)
                grouped_of[g] = grouped
            grouped_words = grouped_of[g][:].bitcast(F32).rearrange("q (n s) -> q n s", s=2)
            xt_ps = psum.tile([P, 2, BANK_TILES * P], F32)
            for i in range(BANK_TILES):
                t = gi * GROUP_TILES + j * BANK_TILES + i
                nc.tensor.transpose(xt_ps[:, 0, i * P : (i + 1) * P], x_words[c][:, t * P : (t + 1) * P], ident_f32[:])
                nc.tensor.transpose(xt_ps[:, 1, i * P : (i + 1) * P], rh_words[c][:, t * P : (t + 1) * P], ident_f32[:])
            nc.scalar.copy(
                out=grouped_words[:, j * BANK_TILES * P : (j + 1) * BANK_TILES * P, :],
                in_=xt_ps[:].rearrange("q s n -> q n s"),
            )

        def quantise(g):
            codes = work.tile([P, GROUP_ROWS], U32, align_bytes=64)
            scales = work.tile([P, GROUP_ROWS], U8, align_bytes=64)
            nc.vector.quantize_mx(out=codes[:].bitcast(FP8X4), scales=scales[:], in_=grouped_of[g][:])
            codes_of[g] = codes
            scales_of[g] = scales

        def multiply(g):
            scaled = work.tile([P, HALVES, GROUP_ROWS], F32)
            for a in range(HALVES):
                acc_ps = psum.tile([P, GROUP_ROWS], F32)
                nc.tensor.matmul_mx(
                    out=acc_ps[:],
                    lhsT=w_codes[:, a * P : (a + 1) * P].bitcast(FP8X4),
                    lhsT_scale=w_scales[:, a * P : (a + 1) * P],
                    rhs=codes_of[g][:].bitcast(FP8X4),
                    rhs_scale=scales_of[g][:],
                    start=True,
                    stop=True,
                )
                nc.scalar.activation(
                    out=scaled[:, a, :],
                    in_=acc_ps[:],
                    func=ACT.Identity,
                    bias=bias_col[:, a : a + 1],
                    scale=cs_col[:, a : a + 1],
                )
            scaled_of[g] = scaled

        def gate_rows(g, j):
            c, gi = divmod(g, CHUNK_GROUPS)
            if j == 0:
                gated = work.tile([P, GROUP_COLS], F32)
                gated_of[g] = gated
            s_ps = psum.tile([P, BANK_TILES * H], F32, bufs=4)
            for i in range(BANK_TILES):
                n0 = (j * BANK_TILES + i) * P
                for a in range(HALVES):
                    block = s_ps[:, i * H + a * P : i * H + (a + 1) * P]
                    if ((j * BANK_TILES + i) * HALVES + a) % MATMUL_EVERY == 0:
                        nc.tensor.matmul(
                            out=block, lhsT=scaled_of[g][:, a, n0 : n0 + P], rhs=ident_f32[:], start=True, stop=True
                        )
                    else:
                        nc.tensor.transpose(block, scaled_of[g][:, a, n0 : n0 + P], ident_f32[:])
            bank = slice(j * BANK_TILES * H, (j + 1) * BANK_TILES * H)
            u_bank = slice(gi * GROUP_COLS + j * BANK_TILES * H, gi * GROUP_COLS + (j + 1) * BANK_TILES * H)
            nc.vector.tensor_tensor(out=gated_of[g][:, bank], in0=s_ps[:], in1=u_sb[c][:, u_bank], op=ALU.mult)

        def finish_rows(g):
            c, gi = divmod(g, CHUNK_GROUPS)
            group_cols = slice(gi * GROUP_COLS, (gi + 1) * GROUP_COLS)
            split = GROUP_COLS - GPSIMD_TILES * H
            for engine, lo, hi in ((nc.vector, 0, split), (nc.gpsimd, split, GROUP_COLS)):
                cols = slice(gi * GROUP_COLS + lo, gi * GROUP_COLS + hi)
                engine.tensor_tensor(
                    out=blend_sb[c][:, cols], in0=gated_of[g][:, lo:hi], in1=blend_sb[c][:, cols], op=ALU.subtract
                )
            nc.sync.dma_start(out=out_rows[:, g * GROUP_COLS : (g + 1) * GROUP_COLS], in_=blend_sb[c][:, group_cols])

        for c in range(LOAD_BUFS):
            load_inputs(c)
        for i in range(-3, GROUPS):
            if 0 <= i + 1 < GROUPS:
                multiply(i + 1)
            if 0 <= i + 2 < GROUPS:
                quantise(i + 2)
            for j in range(GROUP_TILES // BANK_TILES):
                if 0 <= i:
                    gate_rows(i, j)
                if i + 3 < GROUPS:
                    transpose_inputs(i + 3, j)
            if 0 <= i:
                finish_rows(i)
            c, gi = divmod(i + 3, CHUNK_GROUPS)
            if gi == CHUNK_GROUPS - 1 and c + LOAD_BUFS < CHUNKS:
                load_inputs(c + LOAD_BUFS)
